import numpy as np
import ml_dtypes


def mxq(x, axis, fmt="e4m3"):
    dtype, down = {"e4m3": (ml_dtypes.float8_e4m3fn, 7), "e5m2": (ml_dtypes.float8_e5m2, 14)}[fmt]
    v = np.moveaxis(np.asarray(x, np.float32).astype(ml_dtypes.bfloat16).astype(np.float64), axis, -1)
    blocks = v.reshape(v.shape[:-1] + (-1, 32))
    amax = np.abs(blocks).max(-1, keepdims=True)
    byte = np.maximum(np.where(amax > 0, np.frexp(amax)[1] - 1 + 127, 0) - down, 1)
    scale = np.exp2(byte - 127.0)
    codes = (blocks / scale).astype(np.float32).astype(dtype).astype(np.float64)
    return np.moveaxis((codes * scale).reshape(v.shape), -1, axis)


BF16 = ml_dtypes.bfloat16


def bf(x):
    return np.asarray(x, np.float32).astype(BF16)


def f64(x):
    return np.asarray(x).astype(np.float64)


C, H, N, L = 1, 512, 4096, 2048


def setup_inputs():
    return {"W": bf(np.random.standard_normal((C, H, N)) / np.sqrt(N)), "Lambda_im": bf(np.random.uniform(0.0, 2.0 * np.pi, N)), "L": L}


def reference(W, Lambda_im, L):
    pos = np.arange(L, dtype=np.float64)
    S = np.cos(f64(Lambda_im)[:, None] * pos[None, :])
    return mxq(f64(W), 2, "e4m3") @ mxq(S, 0, "e4m3")

@@ -1,0 +1,232 @@
+import math
+from contextlib import ExitStack
+
+import concourse.mybir as mybir
+from concourse.masks import make_identity
+
+F32 = mybir.dt.float32
+BF16 = mybir.dt.bfloat16
+I32 = mybir.dt.int32
+U32 = mybir.dt.uint32
+U8 = mybir.dt.uint8
+FP8X4 = mybir.dt.float8_e4m3fn_x4
+ALU = mybir.AluOpType
+ACT = mybir.ActivationFunctionType
+
+P = 128
+H = 512
+N = 4096
+L_COLS = 2048
+FLOPS = 2 * H * N * L_COLS
+
+PASSES = N // 512
+PLANES = 4 * PASSES
+B = 128
+CHUNKS = L_COLS // B
+ROUNDS = 2
+R_COLS = L_COLS // ROUNDS
+R_CHUNKS = CHUNKS // ROUNDS
+
+U = 32768.0
+C_ALL = U / math.pi
+C1 = 10430.5
+C2 = -0.12164952605962753
+C3 = C_ALL - C1 - C2
+PI_U = math.pi / U
+K_MASK = 0x00FF8000
+PAR_BIT = 0x8000
+
+
+def tile_dlrkernel_kernel(tc, W, Lambda_im, L, out):
+    nc = tc.nc
+    assert L == L_COLS
+    with ExitStack() as ctx:
+        const = ctx.enter_context(tc.tile_pool(name="const", bufs=1))
+        tmp = ctx.enter_context(tc.tile_pool(name="tmp", bufs=2))
+        wstage = ctx.enter_context(tc.tile_pool(name="wstage", bufs=2))
+        zpool = ctx.enter_context(tc.tile_pool(name="zpool", bufs=3))
+        gpool = ctx.enter_context(tc.tile_pool(name="gpool", bufs=2))
+        qpool = ctx.enter_context(tc.tile_pool(name="qpool", bufs=3))
+        opool = ctx.enter_context(tc.tile_pool(name="opool", bufs=4))
+        psum = ctx.enter_context(tc.psum_pool(name="psum", bufs=1))
+
+        lam_bf = const.tile([P, 16, 2], BF16, name="lam_bf")
+        nc.sync.dma_start(out=lam_bf[:], in_=Lambda_im.rearrange("(r p e) -> p r e", p=P, e=2))
+        w_sb = []
+        for m in range(4):
+            w_m = const.tile([P, N], BF16, name="w_sb%d" % m)
+            nc.sync.dma_start(out=w_m[:], in_=W[0, m * P : (m + 1) * P, :])
+            w_sb.append(w_m)
+
+        ident = const.tile([P, P], F32, name="ident")
+        make_identity(nc, ident[:])
+        xi = const.tile([P, B], I32, name="xi")
+        nc.gpsimd.iota(xi[:], pattern=[[1, B]], base=0, channel_multiplier=0)
+        x = const.tile([P, B], F32, name="x")
+        nc.vector.tensor_copy(out=x[:], in_=xi[:])
+
+        def small(dtype, name):
+            return const.tile([P, PLANES], dtype, name=name)
+
+        lam = small(F32, "lam")
+        nc.vector.tensor_copy(out=lam[:], in_=lam_bf[:].rearrange("p r e -> p (r e)"))
+        a1 = small(F32, "a1")
+        nc.vector.tensor_scalar(out=a1[:], in0=lam[:], scalar1=C1, scalar2=None, op0=ALU.mult)
+        mhi = small(I32, "mhi")
+        nc.vector.tensor_copy(out=mhi[:], in_=a1[:])
+        d1 = small(F32, "d1")
+        nc.vector.tensor_tensor(out=d1[:], in0=a1[:], in1=mhi[:], op=ALU.subtract)
+        ml1 = small(F32, "ml1")
+        nc.vector.scalar_tensor_tensor(out=ml1[:], in0=lam[:], scalar=C2, in1=d1[:], op0=ALU.mult, op1=ALU.add)
+        ml = small(F32, "ml")
+        nc.vector.scalar_tensor_tensor(out=ml[:], in0=lam[:], scalar=C3, in1=ml1[:], op0=ALU.mult, op1=ALU.add)
+        mhm = small(I32, "mhm")
+        nc.vector.tensor_single_scalar(out=mhm[:], in_=mhi[:], scalar=0xFFFF, op=ALU.bitwise_and)
+        mh = small(F32, "mh")
+        nc.vector.tensor_copy(out=mh[:], in_=mhm[:])
+        mf = small(F32, "mf")
+        nc.vector.tensor_tensor(out=mf[:], in0=mh[:], in1=ml[:], op=ALU.add)
+        e0 = small(I32, "e0")
+        nc.vector.tensor_scalar(out=e0[:], in0=mh[:], scalar1=float(B), scalar2=None, op0=ALU.mult)
+        em = small(I32, "em")
+        nc.vector.tensor_single_scalar(out=em[:], in_=e0[:], scalar=0xFFFF, op=ALU.bitwise_and)
+        ef = small(F32, "ef")
+        nc.vector.tensor_copy(out=ef[:], in_=em[:])
+        mlb = small(F32, "mlb")
+        nc.vector.tensor_scalar(out=mlb[:], in0=ml[:], scalar1=float(B), scalar2=None, op0=ALU.mult)
+
+        shape3 = [P, PLANES, CHUNKS]
+
+        def phase(dtype, name):
+            return const.tile(shape3, dtype, name=name)
+
+        a_b = x[:, 0:CHUNKS].unsqueeze(1).to_broadcast(shape3)
+        pa = phase(F32, "pa")
+        nc.vector.tensor_tensor(out=pa[:], in0=ef[:].unsqueeze(2).to_broadcast(shape3), in1=a_b, op=ALU.mult)
+        la = phase(F32, "la")
+        nc.vector.tensor_tensor(out=la[:], in0=mlb[:].unsqueeze(2).to_broadcast(shape3), in1=a_b, op=ALU.mult)
+        sm = phase(F32, "sm")
+        nc.vector.tensor_tensor(out=sm[:], in0=pa[:], in1=la[:], op=ALU.add)
+        v1a = phase(I32, "v1a")
+        nc.vector.tensor_scalar(out=v1a[:], in0=sm[:], scalar1=U, scalar2=None, op0=ALU.add)
+        kua = phase(I32, "kua")
+        nc.vector.tensor_single_scalar(out=kua[:], in_=v1a[:], scalar=K_MASK, op=ALU.bitwise_and)
+        da = phase(F32, "da")
+        nc.vector.tensor_tensor(out=da[:], in0=pa[:], in1=kua[:], op=ALU.subtract)
+        ga = phase(F32, "ga")
+        nc.vector.tensor_tensor(out=ga[:], in0=da[:], in1=la[:], op=ALU.add)
+        pba = phase(I32, "pba")
+        nc.vector.tensor_single_scalar(out=pba[:], in_=v1a[:], scalar=PAR_BIT, op=ALU.bitwise_and)
+        sc = phase(F32, "sc")
+        nc.vector.tensor_scalar(
+            out=sc[:], in0=pba[:], scalar1=-2.0 * PI_U / 32768.0, scalar2=PI_U, op0=ALU.mult, op1=ALU.add
+        )
+        bi = phase(F32, "bi")
+        nc.vector.scalar_tensor_tensor(out=bi[:], in0=ga[:], scalar=U / 2.0, in1=sc[:], op0=ALU.add, op1=ALU.mult)
+
+        w_codes = const.tile([P, PASSES, H], U32, name="w_codes", align_bytes=64)
+        w_scales = const.tile([P, PASSES, H], U8, name="w_scales", align_bytes=64)
+        bank = 0
+        for g in range(PASSES):
+            wg = wstage.tile([P, H, 2], F32, name="wg", align_bytes=64)
+            for mp in range(2):
+                xt = psum.tile([P, 2, 2, P], F32, name="xt", tag="bank%d" % bank)
+                bank = (bank + 1) % 8
+                for m2 in range(2):
+                    wv = w_sb[2 * mp + m2][:].bitcast(F32)
+                    for u in range(2):
+                        c0 = 256 * g + 128 * u
+                        nc.tensor.transpose(xt[:, m2, u, :], wv[:, c0 : c0 + P], ident[:])
+                nc.scalar.copy(
+                    out=wg[:, 256 * mp : 256 * (mp + 1), :].rearrange("p (m h) u -> p m h u", m=2),
+                    in_=xt[:].rearrange("p m u h -> p m h u"),
+                )
+            nc.vector.quantize_mx(
+                out=w_codes[:, g, :].bitcast(FP8X4),
+                scales=w_scales[:, g, :],
+                in_=wg[:].rearrange("p h u -> p (h u)").bitcast(BF16),
+            )
+
+        t_tab = const.tile([P, PLANES, B], F32, name="t_tab")
+        s_tab = const.tile([P, PLANES, B], BF16, name="s_tab")
+
+        def build_tables(c):
+            v1 = tmp.tile([P, 4, B], I32, name="v1")
+            for j in range(4):
+                pl = 4 * c + j
+                nc.vector.tensor_scalar(
+                    out=v1[:, j, :], in0=x[:], scalar1=mf[:, pl : pl + 1], scalar2=U / 2.0, op0=ALU.mult, op1=ALU.add
+                )
+            ku = tmp.tile([P, 4, B], I32, name="ku")
+            nc.vector.tensor_single_scalar(out=ku[:], in_=v1[:], scalar=K_MASK, op=ALU.bitwise_and)
+            f1 = tmp.tile([P, 4, B], F32, name="f1")
+            for j in range(4):
+                pl = 4 * c + j
+                nc.vector.scalar_tensor_tensor(
+                    out=f1[:, j, :], in0=x[:], scalar=mh[:, pl : pl + 1], in1=ku[:, j, :], op0=ALU.mult, op1=ALU.subtract
+                )
+                nc.vector.scalar_tensor_tensor(
+                    out=t_tab[:, pl, :], in0=x[:], scalar=ml[:, pl : pl + 1], in1=f1[:, j, :], op0=ALU.mult, op1=ALU.add
+                )
+            pb = tmp.tile([P, 4, B], I32, name="pb")
+            nc.vector.tensor_single_scalar(out=pb[:], in_=v1[:], scalar=PAR_BIT, op=ALU.bitwise_and)
+            nc.vector.tensor_scalar(
+                out=s_tab[:, 4 * c : 4 * c + 4, :], in0=pb[:], scalar1=-1.0 / 16384.0, scalar2=1.0, op0=ALU.mult, op1=ALU.add
+            )
+
+        for r in range(ROUNDS):
+            acc = []
+            for i in range(8):
+                acc_i = psum.tile([P, 512], F32, name="acc", tag="bank%d" % i)
+                acc.append(acc_i)
+            for c in range(PASSES):
+                if r == 0:
+                    build_tables(c)
+                z = zpool.tile([P, 4, R_COLS], BF16, name="z")
+                for j in range(4):
+                    pl = 4 * c + j
+                    for a in range(R_CHUNKS):
+                        ch = r * R_CHUNKS + a
+                        nc.scalar.activation(
+                            out=z[:, j, a * B : (a + 1) * B],
+                            in_=t_tab[:, pl, :],
+                            func=ACT.Sin,
+                            bias=bi[:, pl, ch : ch + 1],
+                            scale=sc[:, pl, ch : ch + 1],
+                        )
+                zv = z[:].rearrange("p j (a b) -> p j a b", b=B)
+                nc.vector.tensor_tensor(
+                    out=zv,
+                    in0=zv,
+                    in1=s_tab[:, 4 * c : 4 * c + 4, :].unsqueeze(2).to_broadcast([P, 4, R_CHUNKS, B]),
+                    op=ALU.mult,
+                )
+                grouped = gpool.tile([P, R_COLS, 4], BF16, name="grouped", align_bytes=64)
+                nc.vector.tensor_copy(
+                    out=grouped[:].rearrange("p (c i) t -> p c t i", i=4),
+                    in_=z[:].rearrange("p t (c i) -> p c t i", i=4),
+                )
+                s_codes = qpool.tile([P, R_COLS], U32, name="s_codes", align_bytes=64)
+                s_scales = qpool.tile([P, R_COLS], U8, name="s_scales", align_bytes=64)
+                nc.vector.quantize_mx(
+                    out=s_codes[:].bitcast(FP8X4),
+                    scales=s_scales[:],
+                    in_=grouped[:].rearrange("p l t -> p (l t)"),
+                )
+                for q in range(2):
+                    for m in range(4):
+                        nc.tensor.matmul_mx(
+                            out=acc[4 * q + m][:],
+                            lhsT=w_codes[:, c, m * P : (m + 1) * P].bitcast(FP8X4),
+                            lhsT_scale=w_scales[:, c, m * P : (m + 1) * P],
+                            rhs=s_codes[:, q * 512 : (q + 1) * 512].bitcast(FP8X4),
+                            rhs_scale=s_scales[:, q * 512 : (q + 1) * 512],
+                            start=(c == 0),
+                            stop=(c == PASSES - 1),
+                        )
+            for q in range(2):
+                for m in range(4):
+                    o_sb = opool.tile([P, 512], F32, name="o_sb")
+                    nc.scalar.copy(out=o_sb[:], in_=acc[4 * q + m][:])
+                    col = r * R_COLS + q * 512
+                    nc.sync.dma_start(out=out[0, m * P : (m + 1) * P, col : col + 512], in_=o_sb[:])

@@ -23,7 +23,7 @@ PASSES = N // 512
 PLANES = 4 * PASSES
 B = 128
 CHUNKS = L_COLS // B
-ROUNDS = 2
+ROUNDS = 4
 R_COLS = L_COLS // ROUNDS
 R_CHUNKS = CHUNKS // ROUNDS
 
@@ -36,6 +36,9 @@ PI_U = math.pi / U
 K_MASK = 0x00FF8000
 PAR_BIT = 0x8000
 
+V_SHARE = (128, 512, 512, 512)
+V_EVAC = ((), (1,), (1,), (1, 3))
+
 
 def tile_dlrkernel_kernel(tc, W, Lambda_im, L, out):
     nc = tc.nc
@@ -43,20 +46,25 @@ def tile_dlrkernel_kernel(tc, W, Lambda_im, L, out):
     with ExitStack() as ctx:
         const = ctx.enter_context(tc.tile_pool(name="const", bufs=1))
         tmp = ctx.enter_context(tc.tile_pool(name="tmp", bufs=2))
-        wstage = ctx.enter_context(tc.tile_pool(name="wstage", bufs=2))
+        wstage = ctx.enter_context(tc.tile_pool(name="wstage", bufs=3))
         zpool = ctx.enter_context(tc.tile_pool(name="zpool", bufs=3))
-        gpool = ctx.enter_context(tc.tile_pool(name="gpool", bufs=2))
-        qpool = ctx.enter_context(tc.tile_pool(name="qpool", bufs=3))
+        gpool = ctx.enter_context(tc.tile_pool(name="gpool", bufs=3))
+        qpool = ctx.enter_context(tc.tile_pool(name="qpool", bufs=4))
         opool = ctx.enter_context(tc.tile_pool(name="opool", bufs=4))
         psum = ctx.enter_context(tc.psum_pool(name="psum", bufs=1))
 
         lam_bf = const.tile([P, 16, 2], BF16, name="lam_bf")
         nc.sync.dma_start(out=lam_bf[:], in_=Lambda_im.rearrange("(r p e) -> p r e", p=P, e=2))
-        w_sb = []
-        for m in range(4):
-            w_m = const.tile([P, N], BF16, name="w_sb%d" % m)
-            nc.sync.dma_start(out=w_m[:], in_=W[0, m * P : (m + 1) * P, :])
-            w_sb.append(w_m)
+        w_view = W[0].rearrange("(m p) n -> p m n", p=P)
+
+        def load_w(g):
+            wld = wstage.tile([P, 4, 512], BF16, name="wld")
+            nc.sync.dma_start(out=wld[:], in_=w_view[:, :, 512 * g : 512 * (g + 1)])
+            return wld
+
+        wlds = {}
+        for g in range(3):
+            wlds[g] = load_w(g)
 
         ident = const.tile([P, P], F32, name="ident")
         make_identity(nc, ident[:])
@@ -68,87 +76,63 @@ def tile_dlrkernel_kernel(tc, W, Lambda_im, L, out):
         def small(dtype, name):
             return const.tile([P, PLANES], dtype, name=name)
 
-        lam = small(F32, "lam")
-        nc.vector.tensor_copy(out=lam[:], in_=lam_bf[:].rearrange("p r e -> p (r e)"))
+        lam = lam_bf[:].rearrange("p r e -> p (r e)")
         a1 = small(F32, "a1")
-        nc.vector.tensor_scalar(out=a1[:], in0=lam[:], scalar1=C1, scalar2=None, op0=ALU.mult)
+        nc.vector.tensor_scalar(out=a1[:], in0=lam, scalar1=C1, scalar2=None, op0=ALU.mult)
         mhi = small(I32, "mhi")
-        nc.vector.tensor_copy(out=mhi[:], in_=a1[:])
+        nc.vector.tensor_scalar(out=mhi[:], in0=lam, scalar1=C1, scalar2=None, op0=ALU.mult)
         d1 = small(F32, "d1")
         nc.vector.tensor_tensor(out=d1[:], in0=a1[:], in1=mhi[:], op=ALU.subtract)
-        ml1 = small(F32, "ml1")
-        nc.vector.scalar_tensor_tensor(out=ml1[:], in0=lam[:], scalar=C2, in1=d1[:], op0=ALU.mult, op1=ALU.add)
-        ml = small(F32, "ml")
-        nc.vector.scalar_tensor_tensor(out=ml[:], in0=lam[:], scalar=C3, in1=ml1[:], op0=ALU.mult, op1=ALU.add)
         mhm = small(I32, "mhm")
         nc.vector.tensor_single_scalar(out=mhm[:], in_=mhi[:], scalar=0xFFFF, op=ALU.bitwise_and)
+        ml1 = small(F32, "ml1")
+        nc.vector.scalar_tensor_tensor(out=ml1[:], in0=lam, scalar=C2, in1=d1[:], op0=ALU.mult, op1=ALU.add)
         mh = small(F32, "mh")
         nc.vector.tensor_copy(out=mh[:], in_=mhm[:])
-        mf = small(F32, "mf")
-        nc.vector.tensor_tensor(out=mf[:], in0=mh[:], in1=ml[:], op=ALU.add)
+        ml = small(F32, "ml")
+        nc.vector.scalar_tensor_tensor(out=ml[:], in0=lam, scalar=C3, in1=ml1[:], op0=ALU.mult, op1=ALU.add)
         e0 = small(I32, "e0")
         nc.vector.tensor_scalar(out=e0[:], in0=mh[:], scalar1=float(B), scalar2=None, op0=ALU.mult)
+        mf = small(F32, "mf")
+        nc.vector.tensor_tensor(out=mf[:], in0=mh[:], in1=ml[:], op=ALU.add)
         em = small(I32, "em")
         nc.vector.tensor_single_scalar(out=em[:], in_=e0[:], scalar=0xFFFF, op=ALU.bitwise_and)
-        ef = small(F32, "ef")
-        nc.vector.tensor_copy(out=ef[:], in_=em[:])
         mlb = small(F32, "mlb")
         nc.vector.tensor_scalar(out=mlb[:], in0=ml[:], scalar1=float(B), scalar2=None, op0=ALU.mult)
+        ef = small(F32, "ef")
+        nc.vector.tensor_copy(out=ef[:], in_=em[:])
 
-        shape3 = [P, PLANES, CHUNKS]
+        sc = const.tile([P, PLANES, CHUNKS], F32, name="sc")
+        bi = const.tile([P, PLANES, CHUNKS], F32, name="bi")
 
-        def phase(dtype, name):
-            return const.tile(shape3, dtype, name=name)
+        def phases(p0, p1, label):
+            shape3 = [P, p1 - p0, CHUNKS]
 
-        a_b = x[:, 0:CHUNKS].unsqueeze(1).to_broadcast(shape3)
-        pa = phase(F32, "pa")
-        nc.vector.tensor_tensor(out=pa[:], in0=ef[:].unsqueeze(2).to_broadcast(shape3), in1=a_b, op=ALU.mult)
-        la = phase(F32, "la")
-        nc.vector.tensor_tensor(out=la[:], in0=mlb[:].unsqueeze(2).to_broadcast(shape3), in1=a_b, op=ALU.mult)
-        sm = phase(F32, "sm")
-        nc.vector.tensor_tensor(out=sm[:], in0=pa[:], in1=la[:], op=ALU.add)
-        v1a = phase(I32, "v1a")
-        nc.vector.tensor_scalar(out=v1a[:], in0=sm[:], scalar1=U, scalar2=None, op0=ALU.add)
-        kua = phase(I32, "kua")
-        nc.vector.tensor_single_scalar(out=kua[:], in_=v1a[:], scalar=K_MASK, op=ALU.bitwise_and)
-        da = phase(F32, "da")
-        nc.vector.tensor_tensor(out=da[:], in0=pa[:], in1=kua[:], op=ALU.subtract)
-        ga = phase(F32, "ga")
-        nc.vector.tensor_tensor(out=ga[:], in0=da[:], in1=la[:], op=ALU.add)
-        pba = phase(I32, "pba")
-        nc.vector.tensor_single_scalar(out=pba[:], in_=v1a[:], scalar=PAR_BIT, op=ALU.bitwise_and)
-        sc = phase(F32, "sc")
-        nc.vector.tensor_scalar(
-            out=sc[:], in0=pba[:], scalar1=-2.0 * PI_U / 32768.0, scalar2=PI_U, op0=ALU.mult, op1=ALU.add
-        )
-        bi = phase(F32, "bi")
-        nc.vector.scalar_tensor_tensor(out=bi[:], in0=ga[:], scalar=U / 2.0, in1=sc[:], op0=ALU.add, op1=ALU.mult)
+            def ph(dtype, name):
+                return const.tile(shape3, dtype, name=name + label)
 
-        w_codes = const.tile([P, PASSES, H], U32, name="w_codes", align_bytes=64)
-        w_scales = const.tile([P, PASSES, H], U8, name="w_scales", align_bytes=64)
-        bank = 0
-        for g in range(PASSES):
-            wg = wstage.tile([P, H, 2], F32, name="wg", align_bytes=64)
-            for mp in range(2):
-                xt = psum.tile([P, 2, 2, P], F32, name="xt", tag="bank%d" % bank)
-                bank = (bank + 1) % 8
-                for m2 in range(2):
-                    wv = w_sb[2 * mp + m2][:].bitcast(F32)
-                    for u in range(2):
-                        c0 = 256 * g + 128 * u
-                        nc.tensor.transpose(xt[:, m2, u, :], wv[:, c0 : c0 + P], ident[:])
-                nc.scalar.copy(
-                    out=wg[:, 256 * mp : 256 * (mp + 1), :].rearrange("p (m h) u -> p m h u", m=2),
-                    in_=xt[:].rearrange("p m u h -> p m h u"),
-                )
-            nc.vector.quantize_mx(
-                out=w_codes[:, g, :].bitcast(FP8X4),
-                scales=w_scales[:, g, :],
-                in_=wg[:].rearrange("p h u -> p (h u)").bitcast(BF16),
+            a_b = x[:, 0:CHUNKS].unsqueeze(1).to_broadcast(shape3)
+            pa = ph(F32, "pa")
+            nc.vector.tensor_tensor(out=pa[:], in0=ef[:, p0:p1].unsqueeze(2).to_broadcast(shape3), in1=a_b, op=ALU.mult)
+            la = ph(F32, "la")
+            nc.vector.tensor_tensor(out=la[:], in0=mlb[:, p0:p1].unsqueeze(2).to_broadcast(shape3), in1=a_b, op=ALU.mult)
+            sm = ph(F32, "sm")
+            v1a = ph(I32, "v1a")
+            nc.vector.scalar_tensor_tensor(out=v1a[:], in0=pa[:], scalar=U, in1=la[:], op0=ALU.add, op1=ALU.add)
+            kua = ph(I32, "kua")
+            nc.vector.tensor_single_scalar(out=kua[:], in_=v1a[:], scalar=K_MASK, op=ALU.bitwise_and)
+            nc.vector.tensor_tensor(out=sm[:], in0=pa[:], in1=kua[:], op=ALU.subtract)
+            nc.vector.tensor_tensor(out=pa[:], in0=sm[:], in1=la[:], op=ALU.add)
+            nc.vector.tensor_single_scalar(out=kua[:], in_=v1a[:], scalar=PAR_BIT, op=ALU.bitwise_and)
+            nc.vector.tensor_scalar(
+                out=sc[:, p0:p1, :], in0=kua[:], scalar1=-2.0 * PI_U / 32768.0, scalar2=PI_U, op0=ALU.mult, op1=ALU.add
+            )
+            nc.vector.scalar_tensor_tensor(
+                out=bi[:, p0:p1, :], in0=pa[:], scalar=U / 2.0, in1=sc[:, p0:p1, :], op0=ALU.add, op1=ALU.mult
             )
 
         t_tab = const.tile([P, PLANES, B], F32, name="t_tab")
-        s_tab = const.tile([P, PLANES, B], BF16, name="s_tab")
+        s_tab = const.tile([P, PASSES, B, 4], BF16, name="s_tab")
 
         def build_tables(c):
             v1 = tmp.tile([P, 4, B], I32, name="v1")
@@ -165,68 +149,143 @@ def tile_dlrkernel_kernel(tc, W, Lambda_im, L, out):
                 nc.vector.scalar_tensor_tensor(
                     out=f1[:, j, :], in0=x[:], scalar=mh[:, pl : pl + 1], in1=ku[:, j, :], op0=ALU.mult, op1=ALU.subtract
                 )
+            for j in range(4):
+                pl = 4 * c + j
                 nc.vector.scalar_tensor_tensor(
                     out=t_tab[:, pl, :], in0=x[:], scalar=ml[:, pl : pl + 1], in1=f1[:, j, :], op0=ALU.mult, op1=ALU.add
                 )
             pb = tmp.tile([P, 4, B], I32, name="pb")
             nc.vector.tensor_single_scalar(out=pb[:], in_=v1[:], scalar=PAR_BIT, op=ALU.bitwise_and)
             nc.vector.tensor_scalar(
-                out=s_tab[:, 4 * c : 4 * c + 4, :], in0=pb[:], scalar1=-1.0 / 16384.0, scalar2=1.0, op0=ALU.mult, op1=ALU.add
+                out=s_tab[:, c, :, :],
+                in0=pb[:].rearrange("p j b -> p b j"),
+                scalar1=-1.0 / 16384.0,
+                scalar2=1.0,
+                op0=ALU.mult,
+                op1=ALU.add,
             )
 
-        for r in range(ROUNDS):
-            acc = []
-            for i in range(8):
-                acc_i = psum.tile([P, 512], F32, name="acc", tag="bank%d" % i)
-                acc.append(acc_i)
-            for c in range(PASSES):
-                if r == 0:
-                    build_tables(c)
-                z = zpool.tile([P, 4, R_COLS], BF16, name="z")
-                for j in range(4):
-                    pl = 4 * c + j
-                    for a in range(R_CHUNKS):
-                        ch = r * R_CHUNKS + a
-                        nc.scalar.activation(
-                            out=z[:, j, a * B : (a + 1) * B],
-                            in_=t_tab[:, pl, :],
-                            func=ACT.Sin,
-                            bias=bi[:, pl, ch : ch + 1],
-                            scale=sc[:, pl, ch : ch + 1],
-                        )
-                zv = z[:].rearrange("p j (a b) -> p j a b", b=B)
-                nc.vector.tensor_tensor(
-                    out=zv,
-                    in0=zv,
-                    in1=s_tab[:, 4 * c : 4 * c + 4, :].unsqueeze(2).to_broadcast([P, 4, R_CHUNKS, B]),
-                    op=ALU.mult,
+        w_codes = const.tile([P, PASSES, H], U32, name="w_codes", align_bytes=64)
+        w_scales = const.tile([P, PASSES, H], U8, name="w_scales", align_bytes=64)
+
+        def prep_w(g):
+            wv = wlds[g][:].rearrange("p m n -> p (m n)").bitcast(F32)
+            wg = wstage.tile([P, H, 2], F32, name="wg", align_bytes=64)
+            for mp in range(2):
+                xt = psum.tile([P, 2, 2, P], F32, name="xt", tag="bank%d" % (4 + (2 * g + mp) % 4))
+                for m2 in range(2):
+                    for u in range(2):
+                        c0 = 256 * (2 * mp + m2) + 128 * u
+                        nc.tensor.transpose(xt[:, m2, u, :], wv[:, c0 : c0 + P], ident[:])
+                nc.scalar.copy(
+                    out=wg[:, 256 * mp : 256 * (mp + 1), :].rearrange("p (m h) u -> p m h u", m=2),
+                    in_=xt[:].rearrange("p m u h -> p m h u"),
                 )
-                grouped = gpool.tile([P, R_COLS, 4], BF16, name="grouped", align_bytes=64)
+            nc.vector.quantize_mx(
+                out=w_codes[:, g, :].bitcast(FP8X4),
+                scales=w_scales[:, g, :],
+                in_=wg[:].rearrange("p h u -> p (h u)").bitcast(BF16),
+            )
+            if g + 3 < PASSES:
+                wlds[g + 3] = load_w(g + 3)
+
+        units = [(r, c) for r in range(ROUNDS) for c in range(PASSES)]
+        acc = {}
+        zs = {}
+        gs = {}
+
+        def sines(u):
+            r, c = units[u]
+            z = zpool.tile([P, 4, R_COLS], BF16, name="z")
+            zs[u] = z
+            for j in range(4):
+                pl = 4 * c + j
+                for a in range(R_CHUNKS):
+                    ch = r * R_CHUNKS + a
+                    nc.scalar.activation(
+                        out=z[:, j, a * B : (a + 1) * B],
+                        in_=t_tab[:, pl, :],
+                        func=ACT.Sin,
+                        bias=bi[:, pl, ch : ch + 1],
+                        scale=sc[:, pl, ch : ch + 1],
+                    )
+
+        def regroup(u):
+            r, c = units[u]
+            z = zs[u]
+            grouped = gpool.tile([P, R_COLS, 4], BF16, name="grouped", align_bytes=64)
+            gs[u] = grouped
+            cv = V_SHARE[r]
+            if cv < R_COLS:
+                nc.scalar.copy(
+                    out=grouped[:, cv:R_COLS, :].rearrange("p (c i) t -> p c t i", i=4),
+                    in_=z[:, :, cv:R_COLS].rearrange("p t (c i) -> p c t i", i=4),
+                )
+            if cv > 0:
                 nc.vector.tensor_copy(
-                    out=grouped[:].rearrange("p (c i) t -> p c t i", i=4),
-                    in_=z[:].rearrange("p t (c i) -> p c t i", i=4),
+                    out=grouped[:, 0:cv, :].rearrange("p (c i) t -> p c t i", i=4),
+                    in_=z[:, :, 0:cv].rearrange("p t (c i) -> p c t i", i=4),
                 )
-                s_codes = qpool.tile([P, R_COLS], U32, name="s_codes", align_bytes=64)
-                s_scales = qpool.tile([P, R_COLS], U8, name="s_scales", align_bytes=64)
-                nc.vector.quantize_mx(
-                    out=s_codes[:].bitcast(FP8X4),
-                    scales=s_scales[:],
-                    in_=grouped[:].rearrange("p l t -> p (l t)"),
+
+        def signs(u):
+            r, c = units[u]
+            gv = gs[u][:].rearrange("p (a b) t -> p a (b t)", b=B)
+            nc.vector.tensor_tensor(
+                out=gv,
+                in0=gv,
+                in1=s_tab[:, c, :, :].rearrange("p b t -> p (b t)").unsqueeze(1).to_broadcast([P, R_CHUNKS, 4 * B]),
+                op=ALU.mult,
+            )
+
+        def quantise_and_multiply(u):
+            r, c = units[u]
+            s_codes = qpool.tile([P, R_COLS], U32, name="s_codes", align_bytes=64)
+            s_scales = qpool.tile([P, R_COLS], U8, name="s_scales", align_bytes=64)
+            nc.vector.quantize_mx(
+                out=s_codes[:].bitcast(FP8X4),
+                scales=s_scales[:],
+                in_=gs[u][:].rearrange("p l t -> p (l t)"),
+            )
+            if c == 0:
+                for m in range(4):
+                    acc_m = psum.tile([P, 512], F32, name="acc", tag="bank%d" % (4 * (r % 2) + m))
+                    acc[m] = acc_m
+            for m in range(4):
+                nc.tensor.matmul_mx(
+                    out=acc[m][:],
+                    lhsT=w_codes[:, c, m * P : (m + 1) * P].bitcast(FP8X4),
+                    lhsT_scale=w_scales[:, c, m * P : (m + 1) * P],
+                    rhs=s_codes[:].bitcast(FP8X4),
+                    rhs_scale=s_scales[:],
+                    start=(c == 0),
+                    stop=(c == PASSES - 1),
                 )
-                for q in range(2):
-                    for m in range(4):
-                        nc.tensor.matmul_mx(
-                            out=acc[4 * q + m][:],
-                            lhsT=w_codes[:, c, m * P : (m + 1) * P].bitcast(FP8X4),
-                            lhsT_scale=w_scales[:, c, m * P : (m + 1) * P],
-                            rhs=s_codes[:, q * 512 : (q + 1) * 512].bitcast(FP8X4),
-                            rhs_scale=s_scales[:, q * 512 : (q + 1) * 512],
-                            start=(c == 0),
-                            stop=(c == PASSES - 1),
-                        )
-            for q in range(2):
+            if c == PASSES - 1:
                 for m in range(4):
                     o_sb = opool.tile([P, 512], F32, name="o_sb")
-                    nc.scalar.copy(out=o_sb[:], in_=acc[4 * q + m][:])
-                    col = r * R_COLS + q * 512
+                    if m in V_EVAC[r]:
+                        nc.vector.tensor_copy(out=o_sb[:], in_=acc[m][:])
+                    else:
+                        nc.scalar.copy(out=o_sb[:], in_=acc[m][:])
+                    col = r * R_COLS
                     nc.sync.dma_start(out=out[0, m * P : (m + 1) * P, col : col + 512], in_=o_sb[:])
+
+        phases(0, 4, "0")
+        build_tables(0)
+        sines(0)
+        prep_w(0)
+        phases(4, PLANES, "1")
+        build_tables(1)
+        n_units = len(units)
+        for u in range(n_units):
+            if u + 1 < n_units:
+                sines(u + 1)
+            regroup(u)
+            if u >= 1:
+                quantise_and_multiply(u - 1)
+            signs(u)
+            if u + 1 < PASSES:
+                prep_w(u + 1)
+            if u + 2 < PASSES:
+                build_tables(u + 2)
+        quantise_and_multiply(n_units - 1)

@@ -23,21 +23,21 @@ PASSES = N // 512
 PLANES = 4 * PASSES
 B = 128
 CHUNKS = L_COLS // B
-ROUNDS = 4
-R_COLS = L_COLS // ROUNDS
-R_CHUNKS = CHUNKS // ROUNDS
 
-U = 32768.0
+U = 131072.0
+U_INT = 131072
 C_ALL = U / math.pi
-C1 = 10430.5
-C2 = -0.12164952605962753
-C3 = C_ALL - C1 - C2
+C1 = 41722.0
+C2 = C_ALL - C1
 PI_U = math.pi / U
-K_MASK = 0x00FF8000
-PAR_BIT = 0x8000
 
-V_SHARE = (128, 512, 512, 512)
-V_EVAC = ((), (1,), (1,), (1, 3))
+ROUNDS = (
+    (0, 512, 128, ()),
+    (512, 512, 512, (1,)),
+    (1024, 512, 512, (1,)),
+    (1536, 256, 256, (1,)),
+    (1792, 256, 256, (1, 3)),
+)
 
 
 def tile_dlrkernel_kernel(tc, W, Lambda_im, L, out):
@@ -46,6 +46,7 @@ def tile_dlrkernel_kernel(tc, W, Lambda_im, L, out):
     with ExitStack() as ctx:
         const = ctx.enter_context(tc.tile_pool(name="const", bufs=1))
         tmp = ctx.enter_context(tc.tile_pool(name="tmp", bufs=2))
+        wload = ctx.enter_context(tc.tile_pool(name="wload", bufs=PASSES))
         wstage = ctx.enter_context(tc.tile_pool(name="wstage", bufs=3))
         zpool = ctx.enter_context(tc.tile_pool(name="zpool", bufs=3))
         gpool = ctx.enter_context(tc.tile_pool(name="gpool", bufs=3))
@@ -56,51 +57,45 @@ def tile_dlrkernel_kernel(tc, W, Lambda_im, L, out):
         lam_bf = const.tile([P, 16, 2], BF16, name="lam_bf")
         nc.sync.dma_start(out=lam_bf[:], in_=Lambda_im.rearrange("(r p e) -> p r e", p=P, e=2))
         w_view = W[0].rearrange("(m p) n -> p m n", p=P)
-
-        def load_w(g):
-            wld = wstage.tile([P, 4, 512], BF16, name="wld")
+        wlds = []
+        for g in range(PASSES):
+            wld = wload.tile([P, 4, 512], BF16, name="wld")
             nc.sync.dma_start(out=wld[:], in_=w_view[:, :, 512 * g : 512 * (g + 1)])
-            return wld
-
-        wlds = {}
-        for g in range(3):
-            wlds[g] = load_w(g)
+            wlds.append(wld)
 
         ident = const.tile([P, P], F32, name="ident")
         make_identity(nc, ident[:])
         xi = const.tile([P, B], I32, name="xi")
-        nc.gpsimd.iota(xi[:], pattern=[[1, B]], base=0, channel_multiplier=0)
+        nc.gpsimd.iota(xi[:], pattern=[[1, B]], base=-(B // 2), channel_multiplier=0)
+        oi = const.tile([P, CHUNKS], I32, name="oi")
+        nc.gpsimd.iota(oi[:], pattern=[[2, CHUNKS]], base=1, channel_multiplier=0)
         x = const.tile([P, B], F32, name="x")
         nc.vector.tensor_copy(out=x[:], in_=xi[:])
+        od = const.tile([P, CHUNKS], F32, name="od")
+        nc.vector.tensor_copy(out=od[:], in_=oi[:])
+        od64 = const.tile([P, CHUNKS], F32, name="od64")
+        nc.vector.tensor_scalar(out=od64[:], in0=oi[:], scalar1=float(B // 2), scalar2=None, op0=ALU.mult)
 
         def small(dtype, name):
             return const.tile([P, PLANES], dtype, name=name)
 
         lam = lam_bf[:].rearrange("p r e -> p (r e)")
-        a1 = small(F32, "a1")
-        nc.vector.tensor_scalar(out=a1[:], in0=lam, scalar1=C1, scalar2=None, op0=ALU.mult)
-        mhi = small(I32, "mhi")
-        nc.vector.tensor_scalar(out=mhi[:], in0=lam, scalar1=C1, scalar2=None, op0=ALU.mult)
-        d1 = small(F32, "d1")
-        nc.vector.tensor_tensor(out=d1[:], in0=a1[:], in1=mhi[:], op=ALU.subtract)
-        mhm = small(I32, "mhm")
-        nc.vector.tensor_single_scalar(out=mhm[:], in_=mhi[:], scalar=0xFFFF, op=ALU.bitwise_and)
-        ml1 = small(F32, "ml1")
-        nc.vector.scalar_tensor_tensor(out=ml1[:], in0=lam, scalar=C2, in1=d1[:], op0=ALU.mult, op1=ALU.add)
-        mh = small(F32, "mh")
-        nc.vector.tensor_copy(out=mh[:], in_=mhm[:])
+        mi = small(I32, "mi")
+        nc.vector.tensor_scalar(out=mi[:], in0=lam, scalar1=C_ALL, scalar2=None, op0=ALU.mult)
+        e1 = small(F32, "e1")
+        nc.vector.scalar_tensor_tensor(out=e1[:], in0=lam, scalar=C1, in1=mi[:], op0=ALU.mult, op1=ALU.subtract)
+        mm = small(I32, "mm")
+        nc.vector.tensor_single_scalar(out=mm[:], in_=mi[:], scalar=2 * U_INT - 1, op=ALU.bitwise_and)
+        ee = small(I32, "ee")
+        nc.vector.tensor_scalar(
+            out=ee[:], in0=mi[:], scalar1=6, scalar2=2 * U_INT - 1, op0=ALU.logical_shift_left, op1=ALU.bitwise_and
+        )
         ml = small(F32, "ml")
-        nc.vector.scalar_tensor_tensor(out=ml[:], in0=lam, scalar=C3, in1=ml1[:], op0=ALU.mult, op1=ALU.add)
-        e0 = small(I32, "e0")
-        nc.vector.tensor_scalar(out=e0[:], in0=mh[:], scalar1=float(B), scalar2=None, op0=ALU.mult)
-        mf = small(F32, "mf")
-        nc.vector.tensor_tensor(out=mf[:], in0=mh[:], in1=ml[:], op=ALU.add)
-        em = small(I32, "em")
-        nc.vector.tensor_single_scalar(out=em[:], in_=e0[:], scalar=0xFFFF, op=ALU.bitwise_and)
-        mlb = small(F32, "mlb")
-        nc.vector.tensor_scalar(out=mlb[:], in0=ml[:], scalar1=float(B), scalar2=None, op0=ALU.mult)
+        nc.vector.scalar_tensor_tensor(out=ml[:], in0=lam, scalar=C2, in1=e1[:], op0=ALU.mult, op1=ALU.add)
+        mh = small(F32, "mh")
+        nc.vector.tensor_copy(out=mh[:], in_=mm[:])
         ef = small(F32, "ef")
-        nc.vector.tensor_copy(out=ef[:], in_=em[:])
+        nc.vector.tensor_copy(out=ef[:], in_=ee[:])
 
         sc = const.tile([P, PLANES, CHUNKS], F32, name="sc")
         bi = const.tile([P, PLANES, CHUNKS], F32, name="bi")
@@ -111,25 +106,33 @@ def tile_dlrkernel_kernel(tc, W, Lambda_im, L, out):
             def ph(dtype, name):
                 return const.tile(shape3, dtype, name=name + label)
 
-            a_b = x[:, 0:CHUNKS].unsqueeze(1).to_broadcast(shape3)
             pa = ph(F32, "pa")
-            nc.vector.tensor_tensor(out=pa[:], in0=ef[:, p0:p1].unsqueeze(2).to_broadcast(shape3), in1=a_b, op=ALU.mult)
+            nc.vector.tensor_tensor(
+                out=pa[:],
+                in0=ef[:, p0:p1].unsqueeze(2).to_broadcast(shape3),
+                in1=od[:].unsqueeze(1).to_broadcast(shape3),
+                op=ALU.mult,
+            )
             la = ph(F32, "la")
-            nc.vector.tensor_tensor(out=la[:], in0=mlb[:, p0:p1].unsqueeze(2).to_broadcast(shape3), in1=a_b, op=ALU.mult)
-            sm = ph(F32, "sm")
+            nc.vector.tensor_tensor(
+                out=la[:],
+                in0=ml[:, p0:p1].unsqueeze(2).to_broadcast(shape3),
+                in1=od64[:].unsqueeze(1).to_broadcast(shape3),
+                op=ALU.mult,
+            )
             v1a = ph(I32, "v1a")
             nc.vector.scalar_tensor_tensor(out=v1a[:], in0=pa[:], scalar=U, in1=la[:], op0=ALU.add, op1=ALU.add)
             kua = ph(I32, "kua")
-            nc.vector.tensor_single_scalar(out=kua[:], in_=v1a[:], scalar=K_MASK, op=ALU.bitwise_and)
-            nc.vector.tensor_tensor(out=sm[:], in0=pa[:], in1=kua[:], op=ALU.subtract)
-            nc.vector.tensor_tensor(out=pa[:], in0=sm[:], in1=la[:], op=ALU.add)
-            nc.vector.tensor_single_scalar(out=kua[:], in_=v1a[:], scalar=PAR_BIT, op=ALU.bitwise_and)
+            nc.vector.tensor_single_scalar(out=kua[:], in_=v1a[:], scalar=0xFFFFFF - (U_INT - 1), op=ALU.bitwise_and)
+            pba = ph(I32, "pba")
+            nc.vector.tensor_single_scalar(out=pba[:], in_=v1a[:], scalar=U_INT, op=ALU.bitwise_and)
+            dd = ph(F32, "dd")
+            nc.vector.tensor_tensor(out=dd[:], in0=pa[:], in1=kua[:], op=ALU.subtract)
             nc.vector.tensor_scalar(
-                out=sc[:, p0:p1, :], in0=kua[:], scalar1=-2.0 * PI_U / 32768.0, scalar2=PI_U, op0=ALU.mult, op1=ALU.add
+                out=sc[:, p0:p1, :], in0=pba[:], scalar1=-2.0 * PI_U / U, scalar2=PI_U, op0=ALU.mult, op1=ALU.add
             )
-            nc.vector.scalar_tensor_tensor(
-                out=bi[:, p0:p1, :], in0=pa[:], scalar=U / 2.0, in1=sc[:, p0:p1, :], op0=ALU.add, op1=ALU.mult
-            )
+            nc.vector.tensor_tensor(out=pa[:], in0=dd[:], in1=la[:], op=ALU.add)
+            nc.vector.tensor_tensor(out=bi[:, p0:p1, :], in0=pa[:], in1=sc[:, p0:p1, :], op=ALU.mult)
 
         t_tab = const.tile([P, PLANES, B], F32, name="t_tab")
         s_tab = const.tile([P, PASSES, B, 4], BF16, name="s_tab")
@@ -139,27 +142,21 @@ def tile_dlrkernel_kernel(tc, W, Lambda_im, L, out):
             for j in range(4):
                 pl = 4 * c + j
                 nc.vector.tensor_scalar(
-                    out=v1[:, j, :], in0=x[:], scalar1=mf[:, pl : pl + 1], scalar2=U / 2.0, op0=ALU.mult, op1=ALU.add
+                    out=v1[:, j, :], in0=x[:], scalar1=mh[:, pl : pl + 1], scalar2=U / 2.0, op0=ALU.mult, op1=ALU.add
                 )
-            ku = tmp.tile([P, 4, B], I32, name="ku")
-            nc.vector.tensor_single_scalar(out=ku[:], in_=v1[:], scalar=K_MASK, op=ALU.bitwise_and)
-            f1 = tmp.tile([P, 4, B], F32, name="f1")
-            for j in range(4):
-                pl = 4 * c + j
-                nc.vector.scalar_tensor_tensor(
-                    out=f1[:, j, :], in0=x[:], scalar=mh[:, pl : pl + 1], in1=ku[:, j, :], op0=ALU.mult, op1=ALU.subtract
-                )
-            for j in range(4):
-                pl = 4 * c + j
-                nc.vector.scalar_tensor_tensor(
-                    out=t_tab[:, pl, :], in0=x[:], scalar=ml[:, pl : pl + 1], in1=f1[:, j, :], op0=ALU.mult, op1=ALU.add
-                )
+            ff = tmp.tile([P, 4, B], I32, name="ff")
+            nc.vector.tensor_single_scalar(out=ff[:], in_=v1[:], scalar=U_INT - 1, op=ALU.bitwise_and)
             pb = tmp.tile([P, 4, B], I32, name="pb")
-            nc.vector.tensor_single_scalar(out=pb[:], in_=v1[:], scalar=PAR_BIT, op=ALU.bitwise_and)
+            nc.vector.tensor_single_scalar(out=pb[:], in_=v1[:], scalar=U_INT, op=ALU.bitwise_and)
+            for j in range(4):
+                pl = 4 * c + j
+                nc.vector.scalar_tensor_tensor(
+                    out=t_tab[:, pl, :], in0=x[:], scalar=ml[:, pl : pl + 1], in1=ff[:, j, :], op0=ALU.mult, op1=ALU.add
+                )
             nc.vector.tensor_scalar(
                 out=s_tab[:, c, :, :],
                 in0=pb[:].rearrange("p j b -> p b j"),
-                scalar1=-1.0 / 16384.0,
+                scalar1=-2.0 / U,
                 scalar2=1.0,
                 op0=ALU.mult,
                 op1=ALU.add,
@@ -167,10 +164,12 @@ def tile_dlrkernel_kernel(tc, W, Lambda_im, L, out):
 
         w_codes = const.tile([P, PASSES, H], U32, name="w_codes", align_bytes=64)
         w_scales = const.tile([P, PASSES, H], U8, name="w_scales", align_bytes=64)
+        wgs = {}
 
-        def prep_w(g):
+        def transpose_w(g):
             wv = wlds[g][:].rearrange("p m n -> p (m n)").bitcast(F32)
             wg = wstage.tile([P, H, 2], F32, name="wg", align_bytes=64)
+            wgs[g] = wg
             for mp in range(2):
                 xt = psum.tile([P, 2, 2, P], F32, name="xt", tag="bank%d" % (4 + (2 * g + mp) % 4))
                 for m2 in range(2):
@@ -181,27 +180,28 @@ def tile_dlrkernel_kernel(tc, W, Lambda_im, L, out):
                     out=wg[:, 256 * mp : 256 * (mp + 1), :].rearrange("p (m h) u -> p m h u", m=2),
                     in_=xt[:].rearrange("p m u h -> p m h u"),
                 )
+
+        def quantise_w(g):
             nc.vector.quantize_mx(
                 out=w_codes[:, g, :].bitcast(FP8X4),
                 scales=w_scales[:, g, :],
-                in_=wg[:].rearrange("p h u -> p (h u)").bitcast(BF16),
+                in_=wgs[g][:].rearrange("p h u -> p (h u)").bitcast(BF16),
             )
-            if g + 3 < PASSES:
-                wlds[g + 3] = load_w(g + 3)
 
-        units = [(r, c) for r in range(ROUNDS) for c in range(PASSES)]
+        units = [(r, c) for r in range(len(ROUNDS)) for c in range(PASSES)]
         acc = {}
         zs = {}
         gs = {}
 
         def sines(u):
             r, c = units[u]
-            z = zpool.tile([P, 4, R_COLS], BF16, name="z")
+            col0, cols = ROUNDS[r][0], ROUNDS[r][1]
+            z = zpool.tile([P, 4, 512], BF16, name="z")
             zs[u] = z
             for j in range(4):
                 pl = 4 * c + j
-                for a in range(R_CHUNKS):
-                    ch = r * R_CHUNKS + a
+                for a in range(cols // B):
+                    ch = col0 // B + a
                     nc.scalar.activation(
                         out=z[:, j, a * B : (a + 1) * B],
                         in_=t_tab[:, pl, :],
@@ -212,14 +212,14 @@ def tile_dlrkernel_kernel(tc, W, Lambda_im, L, out):
 
         def regroup(u):
             r, c = units[u]
+            cols, cv = ROUNDS[r][1], ROUNDS[r][2]
             z = zs[u]
-            grouped = gpool.tile([P, R_COLS, 4], BF16, name="grouped", align_bytes=64)
+            grouped = gpool.tile([P, 512, 4], BF16, name="grouped", align_bytes=64)
             gs[u] = grouped
-            cv = V_SHARE[r]
-            if cv < R_COLS:
+            if cv < cols:
                 nc.scalar.copy(
-                    out=grouped[:, cv:R_COLS, :].rearrange("p (c i) t -> p c t i", i=4),
-                    in_=z[:, :, cv:R_COLS].rearrange("p t (c i) -> p c t i", i=4),
+                    out=grouped[:, cv:cols, :].rearrange("p (c i) t -> p c t i", i=4),
+                    in_=z[:, :, cv:cols].rearrange("p t (c i) -> p c t i", i=4),
                 )
             if cv > 0:
                 nc.vector.tensor_copy(
@@ -229,22 +229,24 @@ def tile_dlrkernel_kernel(tc, W, Lambda_im, L, out):
 
         def signs(u):
             r, c = units[u]
-            gv = gs[u][:].rearrange("p (a b) t -> p a (b t)", b=B)
+            cols = ROUNDS[r][1]
+            gv = gs[u][:, 0:cols, :].rearrange("p (a b) t -> p a (b t)", b=B)
             nc.vector.tensor_tensor(
                 out=gv,
                 in0=gv,
-                in1=s_tab[:, c, :, :].rearrange("p b t -> p (b t)").unsqueeze(1).to_broadcast([P, R_CHUNKS, 4 * B]),
+                in1=s_tab[:, c, :, :].rearrange("p b t -> p (b t)").unsqueeze(1).to_broadcast([P, cols // B, 4 * B]),
                 op=ALU.mult,
             )
 
         def quantise_and_multiply(u):
             r, c = units[u]
-            s_codes = qpool.tile([P, R_COLS], U32, name="s_codes", align_bytes=64)
-            s_scales = qpool.tile([P, R_COLS], U8, name="s_scales", align_bytes=64)
+            col0, cols = ROUNDS[r][0], ROUNDS[r][1]
+            s_codes = qpool.tile([P, 512], U32, name="s_codes", align_bytes=64)
+            s_scales = qpool.tile([P, 512], U8, name="s_scales", align_bytes=64)
             nc.vector.quantize_mx(
-                out=s_codes[:].bitcast(FP8X4),
-                scales=s_scales[:],
-                in_=gs[u][:].rearrange("p l t -> p (l t)"),
+                out=s_codes[:, 0:cols].bitcast(FP8X4),
+                scales=s_scales[:, 0:cols],
+                in_=gs[u][:, 0:cols, :].rearrange("p l t -> p (l t)"),
             )
             if c == 0:
                 for m in range(4):
@@ -252,28 +254,29 @@ def tile_dlrkernel_kernel(tc, W, Lambda_im, L, out):
                     acc[m] = acc_m
             for m in range(4):
                 nc.tensor.matmul_mx(
-                    out=acc[m][:],
+                    out=acc[m][:, 0:cols],
                     lhsT=w_codes[:, c, m * P : (m + 1) * P].bitcast(FP8X4),
                     lhsT_scale=w_scales[:, c, m * P : (m + 1) * P],
-                    rhs=s_codes[:].bitcast(FP8X4),
-                    rhs_scale=s_scales[:],
+                    rhs=s_codes[:, 0:cols].bitcast(FP8X4),
+                    rhs_scale=s_scales[:, 0:cols],
                     start=(c == 0),
                     stop=(c == PASSES - 1),
                 )
             if c == PASSES - 1:
                 for m in range(4):
                     o_sb = opool.tile([P, 512], F32, name="o_sb")
-                    if m in V_EVAC[r]:
-                        nc.vector.tensor_copy(out=o_sb[:], in_=acc[m][:])
+                    if m in ROUNDS[r][3]:
+                        nc.vector.tensor_copy(out=o_sb[:, 0:cols], in_=acc[m][:, 0:cols])
                     else:
-                        nc.scalar.copy(out=o_sb[:], in_=acc[m][:])
-                    col = r * R_COLS
-                    nc.sync.dma_start(out=out[0, m * P : (m + 1) * P, col : col + 512], in_=o_sb[:])
+                        nc.scalar.copy(out=o_sb[:, 0:cols], in_=acc[m][:, 0:cols])
+                    nc.sync.dma_start(out=out[0, m * P : (m + 1) * P, col0 : col0 + cols], in_=o_sb[:, 0:cols])
 
         phases(0, 4, "0")
         build_tables(0)
+        transpose_w(0)
+        transpose_w(1)
         sines(0)
-        prep_w(0)
+        quantise_w(0)
         phases(4, PLANES, "1")
         build_tables(1)
         n_units = len(units)
@@ -285,7 +288,8 @@ def tile_dlrkernel_kernel(tc, W, Lambda_im, L, out):
                 quantise_and_multiply(u - 1)
             signs(u)
             if u + 1 < PASSES:
-                prep_w(u + 1)
+                quantise_w(u + 1)
             if u + 2 < PASSES:
+                transpose_w(u + 2)
                 build_tables(u + 2)
         quantise_and_multiply(n_units - 1)

@@ -32,11 +32,11 @@ C2 = C_ALL - C1
 PI_U = math.pi / U
 
 ROUNDS = (
-    (0, 512, 128, ()),
-    (512, 512, 512, (1,)),
-    (1024, 512, 512, (1,)),
-    (1536, 256, 256, (1,)),
-    (1792, 256, 256, (1, 3)),
+    (0, 512, 128),
+    (512, 512, 480),
+    (1024, 512, 480),
+    (1536, 256, 240),
+    (1792, 256, 240),
 )
 
 
@@ -48,8 +48,8 @@ def tile_dlrkernel_kernel(tc, W, Lambda_im, L, out):
         tmp = ctx.enter_context(tc.tile_pool(name="tmp", bufs=2))
         wload = ctx.enter_context(tc.tile_pool(name="wload", bufs=PASSES))
         wstage = ctx.enter_context(tc.tile_pool(name="wstage", bufs=3))
-        zpool = ctx.enter_context(tc.tile_pool(name="zpool", bufs=3))
-        gpool = ctx.enter_context(tc.tile_pool(name="gpool", bufs=3))
+        zpool = ctx.enter_context(tc.tile_pool(name="zpool", bufs=4))
+        gpool = ctx.enter_context(tc.tile_pool(name="gpool", bufs=4))
         qpool = ctx.enter_context(tc.tile_pool(name="qpool", bufs=4))
         opool = ctx.enter_context(tc.tile_pool(name="opool", bufs=4))
         psum = ctx.enter_context(tc.psum_pool(name="psum", bufs=1))
@@ -210,21 +210,24 @@ def tile_dlrkernel_kernel(tc, W, Lambda_im, L, out):
                         scale=sc[:, pl, ch : ch + 1],
                     )
 
-        def regroup(u):
+        def regroup_scalar(u):
             r, c = units[u]
             cols, cv = ROUNDS[r][1], ROUNDS[r][2]
-            z = zs[u]
             grouped = gpool.tile([P, 512, 4], BF16, name="grouped", align_bytes=64)
             gs[u] = grouped
             if cv < cols:
                 nc.scalar.copy(
                     out=grouped[:, cv:cols, :].rearrange("p (c i) t -> p c t i", i=4),
-                    in_=z[:, :, cv:cols].rearrange("p t (c i) -> p c t i", i=4),
+                    in_=zs[u][:, :, cv:cols].rearrange("p t (c i) -> p c t i", i=4),
                 )
+
+        def regroup_vector(u):
+            r, c = units[u]
+            cv = ROUNDS[r][2]
             if cv > 0:
                 nc.vector.tensor_copy(
-                    out=grouped[:, 0:cv, :].rearrange("p (c i) t -> p c t i", i=4),
-                    in_=z[:, :, 0:cv].rearrange("p t (c i) -> p c t i", i=4),
+                    out=gs[u][:, 0:cv, :].rearrange("p (c i) t -> p c t i", i=4),
+                    in_=zs[u][:, :, 0:cv].rearrange("p t (c i) -> p c t i", i=4),
                 )
 
         def signs(u):
@@ -240,7 +243,7 @@ def tile_dlrkernel_kernel(tc, W, Lambda_im, L, out):
 
         def quantise_and_multiply(u):
             r, c = units[u]
-            col0, cols = ROUNDS[r][0], ROUNDS[r][1]
+            cols = ROUNDS[r][1]
             s_codes = qpool.tile([P, 512], U32, name="s_codes", align_bytes=64)
             s_scales = qpool.tile([P, 512], U8, name="s_scales", align_bytes=64)
             nc.vector.quantize_mx(
@@ -251,10 +254,10 @@ def tile_dlrkernel_kernel(tc, W, Lambda_im, L, out):
             if c == 0:
                 for m in range(4):
                     acc_m = psum.tile([P, 512], F32, name="acc", tag="bank%d" % (4 * (r % 2) + m))
-                    acc[m] = acc_m
+                    acc[(r, m)] = acc_m
             for m in range(4):
                 nc.tensor.matmul_mx(
-                    out=acc[m][:, 0:cols],
+                    out=acc[(r, m)][:, 0:cols],
                     lhsT=w_codes[:, c, m * P : (m + 1) * P].bitcast(FP8X4),
                     lhsT_scale=w_scales[:, c, m * P : (m + 1) * P],
                     rhs=s_codes[:, 0:cols].bitcast(FP8X4),
@@ -262,34 +265,51 @@ def tile_dlrkernel_kernel(tc, W, Lambda_im, L, out):
                     start=(c == 0),
                     stop=(c == PASSES - 1),
                 )
-            if c == PASSES - 1:
-                for m in range(4):
-                    o_sb = opool.tile([P, 512], F32, name="o_sb")
-                    if m in ROUNDS[r][3]:
-                        nc.vector.tensor_copy(out=o_sb[:, 0:cols], in_=acc[m][:, 0:cols])
-                    else:
-                        nc.scalar.copy(out=o_sb[:, 0:cols], in_=acc[m][:, 0:cols])
-                    nc.sync.dma_start(out=out[0, m * P : (m + 1) * P, col0 : col0 + cols], in_=o_sb[:, 0:cols])
 
-        phases(0, 4, "0")
-        build_tables(0)
-        transpose_w(0)
-        transpose_w(1)
-        sines(0)
-        quantise_w(0)
-        phases(4, PLANES, "1")
-        build_tables(1)
+        def empty_bank(r, m, on_vector):
+            col0, cols = ROUNDS[r][0], ROUNDS[r][1]
+            o_sb = opool.tile([P, 512], F32, name="o_sb")
+            if on_vector:
+                nc.vector.tensor_copy(out=o_sb[:, 0:cols], in_=acc[(r, m)][:, 0:cols])
+            else:
+                nc.scalar.copy(out=o_sb[:, 0:cols], in_=acc[(r, m)][:, 0:cols])
+            nc.sync.dma_start(out=out[0, m * P : (m + 1) * P, col0 : col0 + cols], in_=o_sb[:, 0:cols])
+
         n_units = len(units)
-        for u in range(n_units):
-            if u + 1 < n_units:
-                sines(u + 1)
-            regroup(u)
-            if u >= 1:
-                quantise_and_multiply(u - 1)
-            signs(u)
-            if u + 1 < PASSES:
-                quantise_w(u + 1)
-            if u + 2 < PASSES:
-                transpose_w(u + 2)
-                build_tables(u + 2)
-        quantise_and_multiply(n_units - 1)
+        last_round = len(ROUNDS) - 1
+        if True:
+            phases(0, 8, "0")
+            build_tables(0)
+            transpose_w(0)
+            transpose_w(1)
+            sines(0)
+            regroup_scalar(0)
+            build_tables(1)
+            quantise_w(0)
+            phases(8, PLANES, "1")
+            build_tables(2)
+            to_empty = []
+            for u in range(n_units):
+                if u + 1 < n_units:
+                    sines(u + 1)
+                    regroup_scalar(u + 1)
+                if u + 2 < PASSES:
+                    transpose_w(u + 2)
+                regroup_vector(u)
+                if u >= 1:
+                    quantise_and_multiply(u - 1)
+                    r1, c1 = units[u - 1]
+                    if c1 == PASSES - 1:
+                        to_empty.extend([(r1, m) for m in range(4)])
+                signs(u)
+                if len(to_empty) > 0 and units[u][1] >= 1:
+                    r0, m0 = to_empty[0]
+                    to_empty = to_empty[1:]
+                    empty_bank(r0, m0, False)
+                if u + 1 < PASSES:
+                    quantise_w(u + 1)
+                if u + 3 < PASSES:
+                    build_tables(u + 3)
+            quantise_and_multiply(n_units - 1)
+            for m in range(4):
+                empty_bank(last_round, m, m % 2 == 1)

@@ -22,22 +22,17 @@ FLOPS = 2 * H * N * L_COLS
 PASSES = N // 512
 PLANES = 4 * PASSES
 B = 128
-CHUNKS = L_COLS // B
+ROUNDS = 4
 
 U = 131072.0
 U_INT = 131072
+TURN_MASK = 2 * U_INT - 1
 C_ALL = U / math.pi
 C1 = 41722.0
 C2 = C_ALL - C1
 PI_U = math.pi / U
 
-ROUNDS = (
-    (0, 512, 128),
-    (512, 512, 480),
-    (1024, 512, 480),
-    (1536, 256, 240),
-    (1792, 256, 240),
-)
+S_BLOCKS = ((0, 1), (), (), ())
 
 
 def tile_dlrkernel_kernel(tc, W, Lambda_im, L, out):
@@ -46,7 +41,7 @@ def tile_dlrkernel_kernel(tc, W, Lambda_im, L, out):
     with ExitStack() as ctx:
         const = ctx.enter_context(tc.tile_pool(name="const", bufs=1))
         tmp = ctx.enter_context(tc.tile_pool(name="tmp", bufs=2))
-        wload = ctx.enter_context(tc.tile_pool(name="wload", bufs=PASSES))
+        wload = ctx.enter_context(tc.tile_pool(name="wload", bufs=4))
         wstage = ctx.enter_context(tc.tile_pool(name="wstage", bufs=3))
         zpool = ctx.enter_context(tc.tile_pool(name="zpool", bufs=4))
         gpool = ctx.enter_context(tc.tile_pool(name="gpool", bufs=4))
@@ -67,72 +62,97 @@ def tile_dlrkernel_kernel(tc, W, Lambda_im, L, out):
         make_identity(nc, ident[:])
         xi = const.tile([P, B], I32, name="xi")
         nc.gpsimd.iota(xi[:], pattern=[[1, B]], base=-(B // 2), channel_multiplier=0)
-        oi = const.tile([P, CHUNKS], I32, name="oi")
-        nc.gpsimd.iota(oi[:], pattern=[[2, CHUNKS]], base=1, channel_multiplier=0)
+        ri = const.tile([P, 4], I32, name="ri")
+        nc.gpsimd.iota(ri[:], pattern=[[1, 4]], base=0, channel_multiplier=0)
         x = const.tile([P, B], F32, name="x")
         nc.vector.tensor_copy(out=x[:], in_=xi[:])
-        od = const.tile([P, CHUNKS], F32, name="od")
-        nc.vector.tensor_copy(out=od[:], in_=oi[:])
-        od64 = const.tile([P, CHUNKS], F32, name="od64")
-        nc.vector.tensor_scalar(out=od64[:], in0=oi[:], scalar1=float(B // 2), scalar2=None, op0=ALU.mult)
+        rho = const.tile([P, 4], F32, name="rho")
+        nc.vector.tensor_copy(out=rho[:], in_=ri[:])
+        odq = const.tile([P, 4], F32, name="odq")
+        nc.vector.tensor_scalar(out=odq[:], in0=ri[:], scalar1=2.0, scalar2=1.0, op0=ALU.mult, op1=ALU.add)
+        odq64 = const.tile([P, 4], F32, name="odq64")
+        nc.vector.tensor_scalar(out=odq64[:], in0=ri[:], scalar1=128.0, scalar2=64.0, op0=ALU.mult, op1=ALU.add)
 
         def small(dtype, name):
             return const.tile([P, PLANES], dtype, name=name)
 
         lam = lam_bf[:].rearrange("p r e -> p (r e)")
-        mi = small(I32, "mi")
-        nc.vector.tensor_scalar(out=mi[:], in0=lam, scalar1=C_ALL, scalar2=None, op0=ALU.mult)
-        e1 = small(F32, "e1")
-        nc.vector.scalar_tensor_tensor(out=e1[:], in0=lam, scalar=C1, in1=mi[:], op0=ALU.mult, op1=ALU.subtract)
-        mm = small(I32, "mm")
-        nc.vector.tensor_single_scalar(out=mm[:], in_=mi[:], scalar=2 * U_INT - 1, op=ALU.bitwise_and)
+
+        def frequency(k, label):
+            mi = small(I32, "mi" + label)
+            nc.vector.tensor_scalar(out=mi[:], in0=lam, scalar1=k * C_ALL, scalar2=None, op0=ALU.mult)
+            e1 = small(F32, "e1" + label)
+            nc.vector.scalar_tensor_tensor(out=e1[:], in0=lam, scalar=k * C1, in1=mi[:], op0=ALU.mult, op1=ALU.subtract)
+            ml = small(F32, "ml" + label)
+            nc.vector.scalar_tensor_tensor(out=ml[:], in0=lam, scalar=k * C2, in1=e1[:], op0=ALU.mult, op1=ALU.add)
+            mm = small(I32, "mm" + label)
+            nc.vector.tensor_single_scalar(out=mm[:], in_=mi[:], scalar=TURN_MASK, op=ALU.bitwise_and)
+            mh = small(F32, "mh" + label)
+            nc.vector.tensor_copy(out=mh[:], in_=mm[:])
+            return mi, mh, ml
+
+        mi4, mh4, ml4 = frequency(4.0, "4")
+        mi1, mh1, ml1 = frequency(1.0, "1")
         ee = small(I32, "ee")
         nc.vector.tensor_scalar(
-            out=ee[:], in0=mi[:], scalar1=6, scalar2=2 * U_INT - 1, op0=ALU.logical_shift_left, op1=ALU.bitwise_and
+            out=ee[:], in0=mi4[:], scalar1=6, scalar2=TURN_MASK, op0=ALU.logical_shift_left, op1=ALU.bitwise_and
         )
-        ml = small(F32, "ml")
-        nc.vector.scalar_tensor_tensor(out=ml[:], in0=lam, scalar=C2, in1=e1[:], op0=ALU.mult, op1=ALU.add)
-        mh = small(F32, "mh")
-        nc.vector.tensor_copy(out=mh[:], in_=mm[:])
         ef = small(F32, "ef")
         nc.vector.tensor_copy(out=ef[:], in_=ee[:])
 
-        sc = const.tile([P, PLANES, CHUNKS], F32, name="sc")
-        bi = const.tile([P, PLANES, CHUNKS], F32, name="bi")
+        sc = const.tile([P, PLANES, 4, 4], F32, name="sc")
+        bi = const.tile([P, PLANES, 4, 4], F32, name="bi")
 
         def phases(p0, p1, label):
-            shape3 = [P, p1 - p0, CHUNKS]
+            shape2 = [P, p1 - p0, 4]
+            shape4 = [P, p1 - p0, 4, 4]
 
-            def ph(dtype, name):
-                return const.tile(shape3, dtype, name=name + label)
+            def outer(v, tab, name):
+                o = const.tile(shape2, F32, name=name + label)
+                nc.vector.tensor_tensor(
+                    out=o[:],
+                    in0=v[:, p0:p1].unsqueeze(2).to_broadcast(shape2),
+                    in1=tab[:].unsqueeze(1).to_broadcast(shape2),
+                    op=ALU.mult,
+                )
+                return o
 
-            pa = ph(F32, "pa")
-            nc.vector.tensor_tensor(
-                out=pa[:],
-                in0=ef[:, p0:p1].unsqueeze(2).to_broadcast(shape3),
-                in1=od[:].unsqueeze(1).to_broadcast(shape3),
-                op=ALU.mult,
+            def cross(a, b, name):
+                o = const.tile(shape4, F32, name=name + label)
+                nc.vector.tensor_tensor(
+                    out=o[:],
+                    in0=a[:].unsqueeze(3).to_broadcast(shape4),
+                    in1=b[:].unsqueeze(2).to_broadcast(shape4),
+                    op=ALU.add,
+                )
+                return o
+
+            def flat(t):
+                return t.rearrange("p a q r -> p (a q r)")
+
+            pq = outer(ef, odq, "pq")
+            pr = outer(mh1, rho, "pr")
+            lq = outer(ml4, odq64, "lq")
+            lr = outer(ml1, rho, "lr")
+            pa = cross(pq, pr, "pa")
+            la = cross(lq, lr, "la")
+            v1a = const.tile(shape4, I32, name="v1a" + label)
+            nc.vector.scalar_tensor_tensor(
+                out=flat(v1a[:]), in0=flat(pa[:]), scalar=U, in1=flat(la[:]), op0=ALU.add, op1=ALU.add
             )
-            la = ph(F32, "la")
-            nc.vector.tensor_tensor(
-                out=la[:],
-                in0=ml[:, p0:p1].unsqueeze(2).to_broadcast(shape3),
-                in1=od64[:].unsqueeze(1).to_broadcast(shape3),
-                op=ALU.mult,
+            kua = const.tile(shape4, I32, name="kua" + label)
+            nc.vector.tensor_single_scalar(
+                out=flat(kua[:]), in_=flat(v1a[:]), scalar=0xFFFFFF - (U_INT - 1), op=ALU.bitwise_and
             )
-            v1a = ph(I32, "v1a")
-            nc.vector.scalar_tensor_tensor(out=v1a[:], in0=pa[:], scalar=U, in1=la[:], op0=ALU.add, op1=ALU.add)
-            kua = ph(I32, "kua")
-            nc.vector.tensor_single_scalar(out=kua[:], in_=v1a[:], scalar=0xFFFFFF - (U_INT - 1), op=ALU.bitwise_and)
-            pba = ph(I32, "pba")
-            nc.vector.tensor_single_scalar(out=pba[:], in_=v1a[:], scalar=U_INT, op=ALU.bitwise_and)
-            dd = ph(F32, "dd")
-            nc.vector.tensor_tensor(out=dd[:], in0=pa[:], in1=kua[:], op=ALU.subtract)
+            pba = const.tile(shape4, I32, name="pba" + label)
+            nc.vector.tensor_single_scalar(out=flat(pba[:]), in_=flat(v1a[:]), scalar=U_INT, op=ALU.bitwise_and)
+            dd = const.tile(shape4, F32, name="dd" + label)
+            nc.vector.tensor_tensor(out=flat(dd[:]), in0=flat(pa[:]), in1=flat(kua[:]), op=ALU.subtract)
             nc.vector.tensor_scalar(
-                out=sc[:, p0:p1, :], in0=pba[:], scalar1=-2.0 * PI_U / U, scalar2=PI_U, op0=ALU.mult, op1=ALU.add
+                out=flat(sc[:, p0:p1]), in0=flat(pba[:]), scalar1=-2.0 * PI_U / U, scalar2=PI_U, op0=ALU.mult, op1=ALU.add
             )
-            nc.vector.tensor_tensor(out=pa[:], in0=dd[:], in1=la[:], op=ALU.add)
-            nc.vector.tensor_tensor(out=bi[:, p0:p1, :], in0=pa[:], in1=sc[:, p0:p1, :], op=ALU.mult)
+            nc.vector.tensor_tensor(out=flat(pa[:]), in0=flat(dd[:]), in1=flat(la[:]), op=ALU.add)
+            nc.vector.tensor_tensor(out=flat(bi[:, p0:p1]), in0=flat(pa[:]), in1=flat(sc[:, p0:p1]), op=ALU.mult)
 
         t_tab = const.tile([P, PLANES, B], F32, name="t_tab")
         s_tab = const.tile([P, PASSES, B, 4], BF16, name="s_tab")
@@ -142,7 +162,7 @@ def tile_dlrkernel_kernel(tc, W, Lambda_im, L, out):
             for j in range(4):
                 pl = 4 * c + j
                 nc.vector.tensor_scalar(
-                    out=v1[:, j, :], in0=x[:], scalar1=mh[:, pl : pl + 1], scalar2=U / 2.0, op0=ALU.mult, op1=ALU.add
+                    out=v1[:, j, :], in0=x[:], scalar1=mh4[:, pl : pl + 1], scalar2=U / 2.0, op0=ALU.mult, op1=ALU.add
                 )
             ff = tmp.tile([P, 4, B], I32, name="ff")
             nc.vector.tensor_single_scalar(out=ff[:], in_=v1[:], scalar=U_INT - 1, op=ALU.bitwise_and)
@@ -151,7 +171,7 @@ def tile_dlrkernel_kernel(tc, W, Lambda_im, L, out):
             for j in range(4):
                 pl = 4 * c + j
                 nc.vector.scalar_tensor_tensor(
-                    out=t_tab[:, pl, :], in0=x[:], scalar=ml[:, pl : pl + 1], in1=ff[:, j, :], op0=ALU.mult, op1=ALU.add
+                    out=t_tab[:, pl, :], in0=x[:], scalar=ml4[:, pl : pl + 1], in1=ff[:, j, :], op0=ALU.mult, op1=ALU.add
                 )
             nc.vector.tensor_scalar(
                 out=s_tab[:, c, :, :],
@@ -188,128 +208,157 @@ def tile_dlrkernel_kernel(tc, W, Lambda_im, L, out):
                 in_=wgs[g][:].rearrange("p h u -> p (h u)").bitcast(BF16),
             )
 
-        units = [(r, c) for r in range(len(ROUNDS)) for c in range(PASSES)]
+        z_keep = []
+        for q in range(2):
+            zk = const.tile([P, PLANES, 2, B], F32, name="z_keep%d" % q)
+            z_keep.append(zk)
+
+        units = [(q, c) for q in range(ROUNDS) for c in range(PASSES)]
         acc = {}
         zs = {}
         gs = {}
 
-        def sines(u):
-            r, c = units[u]
-            col0, cols = ROUNDS[r][0], ROUNDS[r][1]
-            z = zpool.tile([P, 4, 512], BF16, name="z")
-            zs[u] = z
-            for j in range(4):
-                pl = 4 * c + j
-                for a in range(cols // B):
-                    ch = col0 // B + a
-                    nc.scalar.activation(
-                        out=z[:, j, a * B : (a + 1) * B],
-                        in_=t_tab[:, pl, :],
-                        func=ACT.Sin,
-                        bias=bi[:, pl, ch : ch + 1],
-                        scale=sc[:, pl, ch : ch + 1],
-                    )
-
-        def regroup_scalar(u):
-            r, c = units[u]
-            cols, cv = ROUNDS[r][1], ROUNDS[r][2]
-            grouped = gpool.tile([P, 512, 4], BF16, name="grouped", align_bytes=64)
-            gs[u] = grouped
-            if cv < cols:
-                nc.scalar.copy(
-                    out=grouped[:, cv:cols, :].rearrange("p (c i) t -> p c t i", i=4),
-                    in_=zs[u][:, :, cv:cols].rearrange("p t (c i) -> p c t i", i=4),
-                )
-
-        def regroup_vector(u):
-            r, c = units[u]
-            cv = ROUNDS[r][2]
-            if cv > 0:
-                nc.vector.tensor_copy(
-                    out=gs[u][:, 0:cv, :].rearrange("p (c i) t -> p c t i", i=4),
-                    in_=zs[u][:, :, 0:cv].rearrange("p t (c i) -> p c t i", i=4),
-                )
-
-        def signs(u):
-            r, c = units[u]
-            cols = ROUNDS[r][1]
-            gv = gs[u][:, 0:cols, :].rearrange("p (a b) t -> p a (b t)", b=B)
-            nc.vector.tensor_tensor(
-                out=gv,
-                in0=gv,
-                in1=s_tab[:, c, :, :].rearrange("p b t -> p (b t)").unsqueeze(1).to_broadcast([P, cols // B, 4 * B]),
-                op=ALU.mult,
+        def sine(dst, pl, q, r):
+            nc.scalar.activation(
+                out=dst,
+                in_=t_tab[:, pl, :],
+                func=ACT.Sin,
+                bias=bi[:, pl, q, r : r + 1],
+                scale=sc[:, pl, q, r : r + 1],
             )
 
+        def sines(u):
+            q, c = units[u]
+            if q < 2:
+                zo = z_keep[q][:, 4 * c : 4 * c + 4, :, :]
+            else:
+                zo_t = zpool.tile([P, 4, 2, B], BF16, name="zo")
+                zo = zo_t[:]
+            z0 = zpool.tile([P, 4, B], BF16, name="z0")
+            z2 = zpool.tile([P, 4, B], F32, name="z2")
+            zs[u] = (z0, zo, z2)
+            for j in range(4):
+                for s in range(2):
+                    sine(zo[:, j, s, :], 4 * c + j, q, 1 + 2 * s)
+            half = 64 * (q % 2)
+            src = z_keep[q // 2][:, 4 * c : 4 * c + 4, :, half : half + 64]
+            nc.scalar.activation(
+                out=z2[:].rearrange("p j (i s) -> p j i s", s=2),
+                in_=src.rearrange("p j s i -> p j i s"),
+                func=ACT.Square,
+                scale=math.sqrt(2.0),
+            )
+            for j in range(4):
+                sine(z0[:, j, :], 4 * c + j, q, 0)
+
+        def block(u, r):
+            return gs[u][:, r * B : (r + 1) * B, :].rearrange("p (c i) t -> p c t i", i=4)
+
+        def regroup_block(u, r, on_scalar):
+            z0, zo, z2 = zs[u]
+            if r == 0:
+                src = z0[:].rearrange("p t (c i) -> p c t i", i=4)
+            elif r == 2:
+                src = z2[:].rearrange("p t (c i) -> p c t i", i=4)
+            else:
+                src = zo[:, :, r // 2, :].rearrange("p t (c i) -> p c t i", i=4)
+            if r == 2:
+                if on_scalar:
+                    nc.scalar.add(block(u, r), src, -1.0)
+                else:
+                    nc.vector.tensor_scalar(out=block(u, r), in0=src, scalar1=-1.0, scalar2=None, op0=ALU.add)
+            else:
+                if on_scalar:
+                    nc.scalar.copy(out=block(u, r), in_=src)
+                else:
+                    nc.vector.tensor_copy(out=block(u, r), in_=src)
+
+        def regroup_scalar(u):
+            grouped = gpool.tile([P, 512, 4], BF16, name="grouped", align_bytes=64)
+            gs[u] = grouped
+            for r in S_BLOCKS[units[u][0]]:
+                regroup_block(u, r, True)
+
+        def regroup_vector(u):
+            for r in (1, 3, 0, 2):
+                if r not in S_BLOCKS[units[u][0]]:
+                    regroup_block(u, r, False)
+
+        def signs(u):
+            c = units[u][1]
+            st = s_tab[:, c, :, :].rearrange("p b t -> p (b t)")
+            g01 = gs[u][:, 0 : 2 * B, :].rearrange("p (r b) t -> p r (b t)", r=2)
+            nc.vector.tensor_tensor(out=g01, in0=g01, in1=st.unsqueeze(1).to_broadcast([P, 2, 4 * B]), op=ALU.mult)
+            g3 = gs[u][:, 3 * B : 4 * B, :].rearrange("p b t -> p (b t)")
+            nc.vector.tensor_tensor(out=g3, in0=g3, in1=st, op=ALU.mult)
+
         def quantise_and_multiply(u):
-            r, c = units[u]
-            cols = ROUNDS[r][1]
+            q, c = units[u]
             s_codes = qpool.tile([P, 512], U32, name="s_codes", align_bytes=64)
             s_scales = qpool.tile([P, 512], U8, name="s_scales", align_bytes=64)
             nc.vector.quantize_mx(
-                out=s_codes[:, 0:cols].bitcast(FP8X4),
-                scales=s_scales[:, 0:cols],
-                in_=gs[u][:, 0:cols, :].rearrange("p l t -> p (l t)"),
+                out=s_codes[:].bitcast(FP8X4),
+                scales=s_scales[:],
+                in_=gs[u][:].rearrange("p l t -> p (l t)"),
             )
             if c == 0:
                 for m in range(4):
-                    acc_m = psum.tile([P, 512], F32, name="acc", tag="bank%d" % (4 * (r % 2) + m))
-                    acc[(r, m)] = acc_m
+                    acc_m = psum.tile([P, 512], F32, name="acc", tag="bank%d" % (4 * (q % 2) + m))
+                    acc[(q, m)] = acc_m
             for m in range(4):
                 nc.tensor.matmul_mx(
-                    out=acc[(r, m)][:, 0:cols],
+                    out=acc[(q, m)][:],
                     lhsT=w_codes[:, c, m * P : (m + 1) * P].bitcast(FP8X4),
                     lhsT_scale=w_scales[:, c, m * P : (m + 1) * P],
-                    rhs=s_codes[:, 0:cols].bitcast(FP8X4),
-                    rhs_scale=s_scales[:, 0:cols],
+                    rhs=s_codes[:].bitcast(FP8X4),
+                    rhs_scale=s_scales[:],
                     start=(c == 0),
                     stop=(c == PASSES - 1),
                 )
 
-        def empty_bank(r, m, on_vector):
-            col0, cols = ROUNDS[r][0], ROUNDS[r][1]
+        def empty_bank(q, m, on_vector):
             o_sb = opool.tile([P, 512], F32, name="o_sb")
+            dst = o_sb[:].rearrange("p (i r) -> p i r", r=4)
+            src = acc[(q, m)][:].rearrange("p (r i) -> p i r", r=4)
             if on_vector:
-                nc.vector.tensor_copy(out=o_sb[:, 0:cols], in_=acc[(r, m)][:, 0:cols])
+                nc.vector.tensor_copy(out=dst, in_=src)
             else:
-                nc.scalar.copy(out=o_sb[:, 0:cols], in_=acc[(r, m)][:, 0:cols])
-            nc.sync.dma_start(out=out[0, m * P : (m + 1) * P, col0 : col0 + cols], in_=o_sb[:, 0:cols])
+                nc.scalar.copy(out=dst, in_=src)
+            nc.sync.dma_start(out=out[0, m * P : (m + 1) * P, 512 * q : 512 * (q + 1)], in_=o_sb[:])
 
         n_units = len(units)
-        last_round = len(ROUNDS) - 1
-        if True:
-            phases(0, 8, "0")
-            build_tables(0)
-            transpose_w(0)
-            transpose_w(1)
-            sines(0)
-            regroup_scalar(0)
-            build_tables(1)
-            quantise_w(0)
-            phases(8, PLANES, "1")
-            build_tables(2)
-            to_empty = []
-            for u in range(n_units):
-                if u + 1 < n_units:
-                    sines(u + 1)
-                    regroup_scalar(u + 1)
-                if u + 2 < PASSES:
-                    transpose_w(u + 2)
-                regroup_vector(u)
-                if u >= 1:
-                    quantise_and_multiply(u - 1)
-                    r1, c1 = units[u - 1]
-                    if c1 == PASSES - 1:
-                        to_empty.extend([(r1, m) for m in range(4)])
-                signs(u)
-                if len(to_empty) > 0 and units[u][1] >= 1:
-                    r0, m0 = to_empty[0]
-                    to_empty = to_empty[1:]
-                    empty_bank(r0, m0, False)
-                if u + 1 < PASSES:
-                    quantise_w(u + 1)
-                if u + 3 < PASSES:
-                    build_tables(u + 3)
-            quantise_and_multiply(n_units - 1)
-            for m in range(4):
-                empty_bank(last_round, m, m % 2 == 1)
+        phases(0, 8, "0")
+        build_tables(0)
+        transpose_w(0)
+        transpose_w(1)
+        sines(0)
+        regroup_scalar(0)
+        build_tables(1)
+        quantise_w(0)
+        phases(8, PLANES, "1")
+        build_tables(2)
+        to_empty = []
+        for u in range(n_units):
+            if u + 1 < n_units:
+                sines(u + 1)
+                regroup_scalar(u + 1)
+            if u + 2 < PASSES:
+                transpose_w(u + 2)
+            regroup_vector(u)
+            if u >= 1:
+                quantise_and_multiply(u - 1)
+                q1, c1 = units[u - 1]
+                if c1 == PASSES - 1:
+                    to_empty.extend([(q1, m) for m in range(4)])
+            signs(u)
+            if len(to_empty) > 0 and units[u][1] >= 1:
+                q0, m0 = to_empty[0]
+                to_empty = to_empty[1:]
+                empty_bank(q0, m0, False)
+            if u + 1 < PASSES:
+                quantise_w(u + 1)
+            if u + 3 < PASSES:
+                build_tables(u + 3)
+        quantise_and_multiply(n_units - 1)
+        for m in range(4):
+            empty_bank(ROUNDS - 1, m, m % 2 == 1)

@@ -32,7 +32,9 @@ C1 = 41722.0
 C2 = C_ALL - C1
 PI_U = math.pi / U
 
+A_CLASSES = (0, 1, 3)
 S_BLOCKS = ((0, 1), (), (), ())
+V_BANKS = ((0, 1), (0, 3), (1, 0), (1, 1), (1, 2), (1, 3), (2, 0), (2, 1), (2, 2), (3, 1), (3, 3))
 
 
 def tile_dlrkernel_kernel(tc, W, Lambda_im, L, out):
@@ -40,34 +42,40 @@ def tile_dlrkernel_kernel(tc, W, Lambda_im, L, out):
     assert L == L_COLS
     with ExitStack() as ctx:
         const = ctx.enter_context(tc.tile_pool(name="const", bufs=1))
-        tmp = ctx.enter_context(tc.tile_pool(name="tmp", bufs=2))
-        wload = ctx.enter_context(tc.tile_pool(name="wload", bufs=4))
-        wstage = ctx.enter_context(tc.tile_pool(name="wstage", bufs=3))
-        zpool = ctx.enter_context(tc.tile_pool(name="zpool", bufs=4))
+        zpool = ctx.enter_context(tc.tile_pool(name="zpool", bufs=3))
         gpool = ctx.enter_context(tc.tile_pool(name="gpool", bufs=4))
         qpool = ctx.enter_context(tc.tile_pool(name="qpool", bufs=4))
         opool = ctx.enter_context(tc.tile_pool(name="opool", bufs=4))
         psum = ctx.enter_context(tc.psum_pool(name="psum", bufs=1))
+        early = {}
+        late = {}
 
         lam_bf = const.tile([P, 16, 2], BF16, name="lam_bf")
         nc.sync.dma_start(out=lam_bf[:], in_=Lambda_im.rearrange("(r p e) -> p r e", p=P, e=2))
         w_view = W[0].rearrange("(m p) n -> p m n", p=P)
         wlds = []
-        for g in range(PASSES):
-            wld = wload.tile([P, 4, 512], BF16, name="wld")
-            nc.sync.dma_start(out=wld[:], in_=w_view[:, :, 512 * g : 512 * (g + 1)])
-            wlds.append(wld)
+
+        def load_w():
+            for g in range(PASSES):
+                wld = early["wload"].tile([P, 4, 512], BF16, name="wld")
+                nc.sync.dma_start(out=wld[:], in_=w_view[:, :, 512 * g : 512 * (g + 1)])
+                wlds.append(wld)
 
         ident = const.tile([P, P], F32, name="ident")
         make_identity(nc, ident[:])
         xi = const.tile([P, B], I32, name="xi")
-        nc.gpsimd.iota(xi[:], pattern=[[1, B]], base=-(B // 2), channel_multiplier=0)
+        nc.gpsimd.iota(xi[:], pattern=[[1, 2], [2, B // 2]], base=-(B // 2), channel_multiplier=0)
         ri = const.tile([P, 4], I32, name="ri")
         nc.gpsimd.iota(ri[:], pattern=[[1, 4]], base=0, channel_multiplier=0)
         x = const.tile([P, B], F32, name="x")
         nc.vector.tensor_copy(out=x[:], in_=xi[:])
-        rho = const.tile([P, 4], F32, name="rho")
-        nc.vector.tensor_copy(out=rho[:], in_=ri[:])
+        rho = const.tile([P, 3], F32, name="rho")
+        for k in range(3):
+            nc.vector.memset(rho[:, k : k + 1], float(A_CLASSES[k]))
+        neg_root2 = const.tile([P, 1], F32, name="neg_root2")
+        nc.vector.tensor_scalar(
+            out=neg_root2[:], in0=x[:, 0:1], scalar1=0.0, scalar2=-math.sqrt(2.0), op0=ALU.mult, op1=ALU.add
+        )
         odq = const.tile([P, 4], F32, name="odq")
         nc.vector.tensor_scalar(out=odq[:], in0=ri[:], scalar1=2.0, scalar2=1.0, op0=ALU.mult, op1=ALU.add)
         odq64 = const.tile([P, 4], F32, name="odq64")
@@ -100,15 +108,16 @@ def tile_dlrkernel_kernel(tc, W, Lambda_im, L, out):
         ef = small(F32, "ef")
         nc.vector.tensor_copy(out=ef[:], in_=ee[:])
 
-        sc = const.tile([P, PLANES, 4, 4], F32, name="sc")
-        bi = const.tile([P, PLANES, 4, 4], F32, name="bi")
+        sc = const.tile([P, PLANES, 4, 3], F32, name="sc")
+        bi = const.tile([P, PLANES, 4, 3], F32, name="bi")
 
         def phases(p0, p1, label):
-            shape2 = [P, p1 - p0, 4]
-            shape4 = [P, p1 - p0, 4, 4]
+            shape4 = [P, p1 - p0, 4, 3]
+            pool = early["ph"]
 
-            def outer(v, tab, name):
-                o = const.tile(shape2, F32, name=name + label)
+            def outer(v, tab, width, name):
+                shape2 = [P, p1 - p0, width]
+                o = pool.tile(shape2, F32, name=name + label)
                 nc.vector.tensor_tensor(
                     out=o[:],
                     in0=v[:, p0:p1].unsqueeze(2).to_broadcast(shape2),
@@ -118,7 +127,7 @@ def tile_dlrkernel_kernel(tc, W, Lambda_im, L, out):
                 return o
 
             def cross(a, b, name):
-                o = const.tile(shape4, F32, name=name + label)
+                o = pool.tile(shape4, F32, name=name + label)
                 nc.vector.tensor_tensor(
                     out=o[:],
                     in0=a[:].unsqueeze(3).to_broadcast(shape4),
@@ -130,23 +139,23 @@ def tile_dlrkernel_kernel(tc, W, Lambda_im, L, out):
             def flat(t):
                 return t.rearrange("p a q r -> p (a q r)")
 
-            pq = outer(ef, odq, "pq")
-            pr = outer(mh1, rho, "pr")
-            lq = outer(ml4, odq64, "lq")
-            lr = outer(ml1, rho, "lr")
+            pq = outer(ef, odq, 4, "pq")
+            pr = outer(mh1, rho, 3, "pr")
+            lq = outer(ml4, odq64, 4, "lq")
+            lr = outer(ml1, rho, 3, "lr")
             pa = cross(pq, pr, "pa")
             la = cross(lq, lr, "la")
-            v1a = const.tile(shape4, I32, name="v1a" + label)
+            v1a = pool.tile(shape4, I32, name="v1a" + label)
             nc.vector.scalar_tensor_tensor(
                 out=flat(v1a[:]), in0=flat(pa[:]), scalar=U, in1=flat(la[:]), op0=ALU.add, op1=ALU.add
             )
-            kua = const.tile(shape4, I32, name="kua" + label)
+            kua = pool.tile(shape4, I32, name="kua" + label)
             nc.vector.tensor_single_scalar(
                 out=flat(kua[:]), in_=flat(v1a[:]), scalar=0xFFFFFF - (U_INT - 1), op=ALU.bitwise_and
             )
-            pba = const.tile(shape4, I32, name="pba" + label)
+            pba = pool.tile(shape4, I32, name="pba" + label)
             nc.vector.tensor_single_scalar(out=flat(pba[:]), in_=flat(v1a[:]), scalar=U_INT, op=ALU.bitwise_and)
-            dd = const.tile(shape4, F32, name="dd" + label)
+            dd = pool.tile(shape4, F32, name="dd" + label)
             nc.vector.tensor_tensor(out=flat(dd[:]), in0=flat(pa[:]), in1=flat(kua[:]), op=ALU.subtract)
             nc.vector.tensor_scalar(
                 out=flat(sc[:, p0:p1]), in0=flat(pba[:]), scalar1=-2.0 * PI_U / U, scalar2=PI_U, op0=ALU.mult, op1=ALU.add
@@ -158,6 +167,7 @@ def tile_dlrkernel_kernel(tc, W, Lambda_im, L, out):
         s_tab = const.tile([P, PASSES, B, 4], BF16, name="s_tab")
 
         def build_tables(c):
+            tmp = early["tmp"]
             v1 = tmp.tile([P, 4, B], I32, name="v1")
             for j in range(4):
                 pl = 4 * c + j
@@ -188,7 +198,7 @@ def tile_dlrkernel_kernel(tc, W, Lambda_im, L, out):
 
         def transpose_w(g):
             wv = wlds[g][:].rearrange("p m n -> p (m n)").bitcast(F32)
-            wg = wstage.tile([P, H, 2], F32, name="wg", align_bytes=64)
+            wg = early["wstage"].tile([P, H, 2], F32, name="wg", align_bytes=64)
             wgs[g] = wg
             for mp in range(2):
                 xt = psum.tile([P, 2, 2, P], F32, name="xt", tag="bank%d" % (4 + (2 * g + mp) % 4))
@@ -219,37 +229,60 @@ def tile_dlrkernel_kernel(tc, W, Lambda_im, L, out):
         gs = {}
 
         def sine(dst, pl, q, r):
+            k = A_CLASSES.index(r)
             nc.scalar.activation(
                 out=dst,
                 in_=t_tab[:, pl, :],
                 func=ACT.Sin,
-                bias=bi[:, pl, q, r : r + 1],
-                scale=sc[:, pl, q, r : r + 1],
+                bias=bi[:, pl, q, k : k + 1],
+                scale=sc[:, pl, q, k : k + 1],
             )
+
+        def halved(src, q):
+            v = src.rearrange("p j s (m h i) -> p j s m h i", m=2, h=2)
+            return v[:, :, :, :, q % 2, :].rearrange("p j s m i -> p j s i m")
 
         def sines(u):
             q, c = units[u]
+            pls = slice(4 * c, 4 * c + 4)
             if q < 2:
-                zo = z_keep[q][:, 4 * c : 4 * c + 4, :, :]
+                zo = z_keep[q][:, pls, :, :]
             else:
                 zo_t = zpool.tile([P, 4, 2, B], BF16, name="zo")
                 zo = zo_t[:]
-            z0 = zpool.tile([P, 4, B], BF16, name="z0")
-            z2 = zpool.tile([P, 4, B], F32, name="z2")
+            if q == 1:
+                ze = late["e_keep"][:, pls, :, :]
+            elif q == 0:
+                z0_t = zpool.tile([P, 4, 1, B], BF16, name="z0")
+                z2_t = zpool.tile([P, 4, 1, B], F32, name="z2")
+                ze = None
+            else:
+                ze_t = zpool.tile([P, 4, 2, B], F32, name="ze")
+                ze = ze_t[:]
+            if ze is None:
+                z0, z2 = z0_t[:], z2_t[:]
+            else:
+                z0, z2 = ze[:, :, 0:1, :], ze[:, :, 1:2, :]
             zs[u] = (z0, zo, z2)
             for j in range(4):
                 for s in range(2):
                     sine(zo[:, j, s, :], 4 * c + j, q, 1 + 2 * s)
-            half = 64 * (q % 2)
-            src = z_keep[q // 2][:, 4 * c : 4 * c + 4, :, half : half + 64]
             nc.scalar.activation(
-                out=z2[:].rearrange("p j (i s) -> p j i s", s=2),
-                in_=src.rearrange("p j s i -> p j i s"),
+                out=z2[:, :, 0, :].rearrange("p j (s i m) -> p j s i m", s=2, m=2),
+                in_=halved(z_keep[q // 2][:, pls, :, :], q),
                 func=ACT.Square,
                 scale=math.sqrt(2.0),
             )
-            for j in range(4):
-                sine(z0[:, j, :], 4 * c + j, q, 0)
+            if q < 2:
+                for j in range(4):
+                    sine(z0[:, j, 0, :], 4 * c + j, q, 0)
+            else:
+                src = halved(late["e_keep"][:, pls, :, :], q)
+                dst = z0[:, :, 0, :].rearrange("p j (s i m) -> p j s i m", s=2, m=2)
+                nc.scalar.activation(out=dst[:, :, 0:1], in_=src[:, :, 0:1], func=ACT.Square, scale=math.sqrt(2.0))
+                nc.scalar.activation(
+                    out=dst[:, :, 1:2], in_=src[:, :, 1:2], func=ACT.Square, scale=math.sqrt(2.0), bias=neg_root2[:]
+                )
 
         def block(u, r):
             return gs[u][:, r * B : (r + 1) * B, :].rearrange("p (c i) t -> p c t i", i=4)
@@ -257,12 +290,12 @@ def tile_dlrkernel_kernel(tc, W, Lambda_im, L, out):
         def regroup_block(u, r, on_scalar):
             z0, zo, z2 = zs[u]
             if r == 0:
-                src = z0[:].rearrange("p t (c i) -> p c t i", i=4)
+                src = z0[:, :, 0, :].rearrange("p t (c i) -> p c t i", i=4)
             elif r == 2:
-                src = z2[:].rearrange("p t (c i) -> p c t i", i=4)
+                src = z2[:, :, 0, :].rearrange("p t (c i) -> p c t i", i=4)
             else:
                 src = zo[:, :, r // 2, :].rearrange("p t (c i) -> p c t i", i=4)
-            if r == 2:
+            if r == 2 or (r == 0 and units[u][0] >= 2):
                 if on_scalar:
                     nc.scalar.add(block(u, r), src, -1.0)
                 else:
@@ -285,12 +318,17 @@ def tile_dlrkernel_kernel(tc, W, Lambda_im, L, out):
                     regroup_block(u, r, False)
 
         def signs(u):
-            c = units[u][1]
+            q, c = units[u]
             st = s_tab[:, c, :, :].rearrange("p b t -> p (b t)")
-            g01 = gs[u][:, 0 : 2 * B, :].rearrange("p (r b) t -> p r (b t)", r=2)
-            nc.vector.tensor_tensor(out=g01, in0=g01, in1=st.unsqueeze(1).to_broadcast([P, 2, 4 * B]), op=ALU.mult)
-            g3 = gs[u][:, 3 * B : 4 * B, :].rearrange("p b t -> p (b t)")
-            nc.vector.tensor_tensor(out=g3, in0=g3, in1=st, op=ALU.mult)
+            two = st.unsqueeze(1).to_broadcast([P, 2, 4 * B])
+            if q < 2:
+                g01 = gs[u][:, 0 : 2 * B, :].rearrange("p (r b) t -> p r (b t)", r=2)
+                nc.vector.tensor_tensor(out=g01, in0=g01, in1=two, op=ALU.mult)
+                g3 = gs[u][:, 3 * B : 4 * B, :].rearrange("p b t -> p (b t)")
+                nc.vector.tensor_tensor(out=g3, in0=g3, in1=st, op=ALU.mult)
+            else:
+                g13 = gs[u][:].rearrange("p (k r b) t -> p k r (b t)", k=2, r=2)[:, :, 1, :]
+                nc.vector.tensor_tensor(out=g13, in0=g13, in1=two, op=ALU.mult)
 
         def quantise_and_multiply(u):
             q, c = units[u]
@@ -318,8 +356,8 @@ def tile_dlrkernel_kernel(tc, W, Lambda_im, L, out):
 
         def empty_bank(q, m, on_vector):
             o_sb = opool.tile([P, 512], F32, name="o_sb")
-            dst = o_sb[:].rearrange("p (i r) -> p i r", r=4)
-            src = acc[(q, m)][:].rearrange("p (r i) -> p i r", r=4)
+            dst = o_sb[:].rearrange("p (i s r) -> p i s r", s=2, r=4)
+            src = acc[(q, m)][:].rearrange("p (r s i) -> p i s r", r=4, s=2)
             if on_vector:
                 nc.vector.tensor_copy(out=dst, in_=src)
             else:
@@ -327,18 +365,10 @@ def tile_dlrkernel_kernel(tc, W, Lambda_im, L, out):
             nc.sync.dma_start(out=out[0, m * P : (m + 1) * P, 512 * q : 512 * (q + 1)], in_=o_sb[:])
 
         n_units = len(units)
-        phases(0, 8, "0")
-        build_tables(0)
-        transpose_w(0)
-        transpose_w(1)
-        sines(0)
-        regroup_scalar(0)
-        build_tables(1)
-        quantise_w(0)
-        phases(8, PLANES, "1")
-        build_tables(2)
         to_empty = []
-        for u in range(n_units):
+        emptied = [0]
+
+        def iteration(u):
             if u + 1 < n_units:
                 sines(u + 1)
                 regroup_scalar(u + 1)
@@ -351,14 +381,38 @@ def tile_dlrkernel_kernel(tc, W, Lambda_im, L, out):
                 if c1 == PASSES - 1:
                     to_empty.extend([(q1, m) for m in range(4)])
             signs(u)
-            if len(to_empty) > 0 and units[u][1] >= 1:
-                q0, m0 = to_empty[0]
-                to_empty = to_empty[1:]
-                empty_bank(q0, m0, False)
+            if len(to_empty) > emptied[0] and units[u][1] >= 1:
+                q0, m0 = to_empty[emptied[0]]
+                emptied[0] = emptied[0] + 1
+                empty_bank(q0, m0, (q0, m0) in V_BANKS)
             if u + 1 < PASSES:
                 quantise_w(u + 1)
             if u + 3 < PASSES:
                 build_tables(u + 3)
-        quantise_and_multiply(n_units - 1)
-        for m in range(4):
-            empty_bank(ROUNDS - 1, m, m % 2 == 1)
+
+        with ExitStack() as first:
+            early["tmp"] = first.enter_context(tc.tile_pool(name="tmp", bufs=2))
+            early["ph"] = first.enter_context(tc.tile_pool(name="ph", bufs=1))
+            early["wload"] = first.enter_context(tc.tile_pool(name="wload", bufs=4))
+            early["wstage"] = first.enter_context(tc.tile_pool(name="wstage", bufs=3))
+            load_w()
+            phases(0, 8, "0")
+            build_tables(0)
+            transpose_w(0)
+            transpose_w(1)
+            sines(0)
+            regroup_scalar(0)
+            build_tables(1)
+            quantise_w(0)
+            phases(8, PLANES, "1")
+            build_tables(2)
+            for u in range(PASSES - 1):
+                iteration(u)
+        with tc.tile_pool(name="ekeep", bufs=1) as ekeep:
+            e_keep = ekeep.tile([P, PLANES, 2, B], F32, name="e_keep")
+            late["e_keep"] = e_keep
+            for u in range(PASSES - 1, n_units):
+                iteration(u)
+            quantise_and_multiply(n_units - 1)
+            for m in range(4):
+                empty_bank(ROUNDS - 1, m, (ROUNDS - 1, m) in V_BANKS)

@@ -33,8 +33,9 @@ C2 = C_ALL - C1
 PI_U = math.pi / U
 
 A_CLASSES = (0, 1, 3)
-S_BLOCKS = ((0, 1), (), (), ())
-V_BANKS = ((0, 1), (0, 3), (1, 0), (1, 1), (1, 2), (1, 3), (2, 0), (2, 1), (2, 2), (3, 1), (3, 3))
+S_BLOCKS = ((), (), (), ())
+V_BANKS = ((3, 1), (3, 3))
+LEAD = 6
 
 
 def tile_dlrkernel_kernel(tc, W, Lambda_im, L, out):
@@ -42,10 +43,10 @@ def tile_dlrkernel_kernel(tc, W, Lambda_im, L, out):
     assert L == L_COLS
     with ExitStack() as ctx:
         const = ctx.enter_context(tc.tile_pool(name="const", bufs=1))
-        zpool = ctx.enter_context(tc.tile_pool(name="zpool", bufs=3))
-        gpool = ctx.enter_context(tc.tile_pool(name="gpool", bufs=4))
+        zpool = ctx.enter_context(tc.tile_pool(name="zpool", bufs=LEAD + 1))
+        gpool = ctx.enter_context(tc.tile_pool(name="gpool", bufs=3))
         qpool = ctx.enter_context(tc.tile_pool(name="qpool", bufs=4))
-        opool = ctx.enter_context(tc.tile_pool(name="opool", bufs=4))
+        opool = ctx.enter_context(tc.tile_pool(name="opool", bufs=3))
         psum = ctx.enter_context(tc.psum_pool(name="psum", bufs=1))
         early = {}
         late = {}
@@ -245,24 +246,18 @@ def tile_dlrkernel_kernel(tc, W, Lambda_im, L, out):
         def sines(u):
             q, c = units[u]
             pls = slice(4 * c, 4 * c + 4)
-            if q < 2:
-                zo = z_keep[q][:, pls, :, :]
+            if q != 1:
+                zh = zpool.tile([P, 4, 2, B], BF16, name="zh")
+                zf = zpool.tile([P, 4, 2, B], F32, name="zf")
+            if q == 0:
+                zo = z_keep[0][:, pls, :, :]
+                z0, z2 = zh[:, :, 0:1, :], zf[:, :, 0:1, :]
+            elif q == 1:
+                zo = z_keep[1][:, pls, :, :]
+                z0, z2 = late["e_keep"][:, pls, 0:1, :], late["e_keep"][:, pls, 1:2, :]
             else:
-                zo_t = zpool.tile([P, 4, 2, B], BF16, name="zo")
-                zo = zo_t[:]
-            if q == 1:
-                ze = late["e_keep"][:, pls, :, :]
-            elif q == 0:
-                z0_t = zpool.tile([P, 4, 1, B], BF16, name="z0")
-                z2_t = zpool.tile([P, 4, 1, B], F32, name="z2")
-                ze = None
-            else:
-                ze_t = zpool.tile([P, 4, 2, B], F32, name="ze")
-                ze = ze_t[:]
-            if ze is None:
-                z0, z2 = z0_t[:], z2_t[:]
-            else:
-                z0, z2 = ze[:, :, 0:1, :], ze[:, :, 1:2, :]
+                zo = zh[:]
+                z0, z2 = zf[:, :, 0:1, :], zf[:, :, 1:2, :]
             zs[u] = (z0, zo, z2)
             for j in range(4):
                 for s in range(2):
@@ -369,11 +364,9 @@ def tile_dlrkernel_kernel(tc, W, Lambda_im, L, out):
         emptied = [0]
 
         def iteration(u):
-            if u + 1 < n_units:
-                sines(u + 1)
-                regroup_scalar(u + 1)
-            if u + 2 < PASSES:
-                transpose_w(u + 2)
+            if u + LEAD < n_units:
+                sines(u + LEAD)
+            regroup_scalar(u)
             regroup_vector(u)
             if u >= 1:
                 quantise_and_multiply(u - 1)
@@ -385,33 +378,33 @@ def tile_dlrkernel_kernel(tc, W, Lambda_im, L, out):
                 q0, m0 = to_empty[emptied[0]]
                 emptied[0] = emptied[0] + 1
                 empty_bank(q0, m0, (q0, m0) in V_BANKS)
-            if u + 1 < PASSES:
-                quantise_w(u + 1)
-            if u + 3 < PASSES:
-                build_tables(u + 3)
 
         with ExitStack() as first:
             early["tmp"] = first.enter_context(tc.tile_pool(name="tmp", bufs=2))
             early["ph"] = first.enter_context(tc.tile_pool(name="ph", bufs=1))
-            early["wload"] = first.enter_context(tc.tile_pool(name="wload", bufs=4))
+            early["wload"] = first.enter_context(tc.tile_pool(name="wload", bufs=3))
             early["wstage"] = first.enter_context(tc.tile_pool(name="wstage", bufs=3))
             load_w()
             phases(0, 8, "0")
             build_tables(0)
             transpose_w(0)
-            transpose_w(1)
             sines(0)
-            regroup_scalar(0)
             build_tables(1)
-            quantise_w(0)
+            transpose_w(1)
+            sines(1)
             phases(8, PLANES, "1")
-            build_tables(2)
-            for u in range(PASSES - 1):
-                iteration(u)
+            for c in range(2, PASSES):
+                build_tables(c)
+                transpose_w(c)
+                if c < LEAD:
+                    sines(c)
+                quantise_w(c - 2)
+            quantise_w(PASSES - 2)
+            quantise_w(PASSES - 1)
         with tc.tile_pool(name="ekeep", bufs=1) as ekeep:
             e_keep = ekeep.tile([P, PLANES, 2, B], F32, name="e_keep")
             late["e_keep"] = e_keep
-            for u in range(PASSES - 1, n_units):
+            for u in range(n_units):
                 iteration(u)
             quantise_and_multiply(n_units - 1)
             for m in range(4):

@@ -33,7 +33,7 @@ C2 = C_ALL - C1
 PI_U = math.pi / U
 
 A_CLASSES = (0, 1, 3)
-S_BLOCKS = ((), (), (), ())
+S_UNITS = ((1, 0), (1, 2), (1, 4), (1, 6))
 V_BANKS = ((3, 1), (3, 3))
 LEAD = 6
 
@@ -228,6 +228,12 @@ def tile_dlrkernel_kernel(tc, W, Lambda_im, L, out):
         acc = {}
         zs = {}
         gs = {}
+        ahead = {}
+
+        def share(u):
+            if units[u] in S_UNITS:
+                return (0, 1)
+            return ()
 
         def sine(dst, pl, q, r):
             k = A_CLASSES.index(r)
@@ -246,17 +252,20 @@ def tile_dlrkernel_kernel(tc, W, Lambda_im, L, out):
         def sines(u):
             q, c = units[u]
             pls = slice(4 * c, 4 * c + 4)
+            if q != 1 or len(share(u)) > 0:
+                zh = zpool.tile([P, 8 * B], BF16, name="zh", align_bytes=64)
             if q != 1:
-                zh = zpool.tile([P, 4, 2, B], BF16, name="zh")
                 zf = zpool.tile([P, 4, 2, B], F32, name="zf")
+            if len(share(u)) > 0:
+                ahead[u] = zh[:].rearrange("p (r b t) -> p r b t", r=2, t=4)
             if q == 0:
                 zo = z_keep[0][:, pls, :, :]
-                z0, z2 = zh[:, :, 0:1, :], zf[:, :, 0:1, :]
+                z0, z2 = zh[:].rearrange("p (j s b) -> p j s b", j=4, s=2)[:, :, 0:1, :], zf[:, :, 0:1, :]
             elif q == 1:
                 zo = z_keep[1][:, pls, :, :]
                 z0, z2 = late["e_keep"][:, pls, 0:1, :], late["e_keep"][:, pls, 1:2, :]
             else:
-                zo = zh[:]
+                zo = zh[:].rearrange("p (j s b) -> p j s b", j=4, s=2)
                 z0, z2 = zf[:, :, 0:1, :], zf[:, :, 1:2, :]
             zs[u] = (z0, zo, z2)
             for j in range(4):
@@ -271,6 +280,8 @@ def tile_dlrkernel_kernel(tc, W, Lambda_im, L, out):
             if q < 2:
                 for j in range(4):
                     sine(z0[:, j, 0, :], 4 * c + j, q, 0)
+                for r in reversed(share(u)):
+                    regroup_block(u, r, True)
             else:
                 src = halved(late["e_keep"][:, pls, :, :], q)
                 dst = z0[:, :, 0, :].rearrange("p j (s i m) -> p j s i m", s=2, m=2)
@@ -280,6 +291,8 @@ def tile_dlrkernel_kernel(tc, W, Lambda_im, L, out):
                 )
 
         def block(u, r):
+            if r in share(u):
+                return ahead[u][:, r, :, :].rearrange("p (c i) t -> p c t i", i=4)
             return gs[u][:, r * B : (r + 1) * B, :].rearrange("p (c i) t -> p c t i", i=4)
 
         def regroup_block(u, r, on_scalar):
@@ -304,12 +317,10 @@ def tile_dlrkernel_kernel(tc, W, Lambda_im, L, out):
         def regroup_scalar(u):
             grouped = gpool.tile([P, 512, 4], BF16, name="grouped", align_bytes=64)
             gs[u] = grouped
-            for r in S_BLOCKS[units[u][0]]:
-                regroup_block(u, r, True)
 
         def regroup_vector(u):
             for r in (1, 3, 0, 2):
-                if r not in S_BLOCKS[units[u][0]]:
+                if r not in share(u):
                     regroup_block(u, r, False)
 
         def signs(u):
@@ -317,7 +328,10 @@ def tile_dlrkernel_kernel(tc, W, Lambda_im, L, out):
             st = s_tab[:, c, :, :].rearrange("p b t -> p (b t)")
             two = st.unsqueeze(1).to_broadcast([P, 2, 4 * B])
             if q < 2:
-                g01 = gs[u][:, 0 : 2 * B, :].rearrange("p (r b) t -> p r (b t)", r=2)
+                if len(share(u)) > 0:
+                    g01 = ahead[u].rearrange("p r b t -> p r (b t)")
+                else:
+                    g01 = gs[u][:, 0 : 2 * B, :].rearrange("p (r b) t -> p r (b t)", r=2)
                 nc.vector.tensor_tensor(out=g01, in0=g01, in1=two, op=ALU.mult)
                 g3 = gs[u][:, 3 * B : 4 * B, :].rearrange("p b t -> p (b t)")
                 nc.vector.tensor_tensor(out=g3, in0=g3, in1=st, op=ALU.mult)
@@ -329,11 +343,23 @@ def tile_dlrkernel_kernel(tc, W, Lambda_im, L, out):
             q, c = units[u]
             s_codes = qpool.tile([P, 512], U32, name="s_codes", align_bytes=64)
             s_scales = qpool.tile([P, 512], U8, name="s_scales", align_bytes=64)
-            nc.vector.quantize_mx(
-                out=s_codes[:].bitcast(FP8X4),
-                scales=s_scales[:],
-                in_=gs[u][:].rearrange("p l t -> p (l t)"),
-            )
+            if len(share(u)) > 0:
+                nc.vector.quantize_mx(
+                    out=s_codes[:, 0 : 2 * B].bitcast(FP8X4),
+                    scales=s_scales[:, 0 : 2 * B],
+                    in_=ahead[u].rearrange("p r b t -> p (r b t)"),
+                )
+                nc.vector.quantize_mx(
+                    out=s_codes[:, 2 * B : 4 * B].bitcast(FP8X4),
+                    scales=s_scales[:, 2 * B : 4 * B],
+                    in_=gs[u][:, 2 * B : 4 * B, :].rearrange("p l t -> p (l t)"),
+                )
+            else:
+                nc.vector.quantize_mx(
+                    out=s_codes[:].bitcast(FP8X4),
+                    scales=s_scales[:],
+                    in_=gs[u][:].rearrange("p l t -> p (l t)"),
+                )
             if c == 0:
                 for m in range(4):
                     acc_m = psum.tile([P, 512], F32, name="acc", tag="bank%d" % (4 * (q % 2) + m))

@@ -22,18 +22,20 @@ FLOPS = 2 * H * N * L_COLS
 PASSES = N // 512
 PLANES = 4 * PASSES
 B = 128
+HALF = B // 2
 ROUNDS = 4
 
 U = 131072.0
 U_INT = 131072
 TURN_MASK = 2 * U_INT - 1
+TURN_SHIFT = 14
 C_ALL = U / math.pi
 C1 = 41722.0
 C2 = C_ALL - C1
 PI_U = math.pi / U
 
 A_CLASSES = (0, 1, 3)
-S_UNITS = ((1, 0), (1, 2), (1, 4), (1, 6))
+S_UNITS = ()
 V_BANKS = ((3, 1), (3, 3))
 LEAD = 6
 
@@ -64,23 +66,23 @@ def tile_dlrkernel_kernel(tc, W, Lambda_im, L, out):
 
         ident = const.tile([P, P], F32, name="ident")
         make_identity(nc, ident[:])
-        xi = const.tile([P, B], I32, name="xi")
-        nc.gpsimd.iota(xi[:], pattern=[[1, 2], [2, B // 2]], base=-(B // 2), channel_multiplier=0)
+        xi = const.tile([P, HALF], I32, name="xi")
+        nc.gpsimd.iota(xi[:], pattern=[[2, 2], [4, HALF // 2]], base=1, channel_multiplier=0)
         ri = const.tile([P, 4], I32, name="ri")
         nc.gpsimd.iota(ri[:], pattern=[[1, 4]], base=0, channel_multiplier=0)
-        x = const.tile([P, B], F32, name="x")
+        x = const.tile([P, HALF], F32, name="x")
         nc.vector.tensor_copy(out=x[:], in_=xi[:])
         rho = const.tile([P, 3], F32, name="rho")
         for k in range(3):
-            nc.vector.memset(rho[:, k : k + 1], float(A_CLASSES[k]))
+            nc.vector.memset(rho[:, k : k + 1], float(A_CLASSES[k] - 2))
         neg_root2 = const.tile([P, 1], F32, name="neg_root2")
         nc.vector.tensor_scalar(
             out=neg_root2[:], in0=x[:, 0:1], scalar1=0.0, scalar2=-math.sqrt(2.0), op0=ALU.mult, op1=ALU.add
         )
         odq = const.tile([P, 4], F32, name="odq")
         nc.vector.tensor_scalar(out=odq[:], in0=ri[:], scalar1=2.0, scalar2=1.0, op0=ALU.mult, op1=ALU.add)
-        odq64 = const.tile([P, 4], F32, name="odq64")
-        nc.vector.tensor_scalar(out=odq64[:], in0=ri[:], scalar1=128.0, scalar2=64.0, op0=ALU.mult, op1=ALU.add)
+        odq128 = const.tile([P, 4], F32, name="odq128")
+        nc.vector.tensor_scalar(out=odq128[:], in0=ri[:], scalar1=256.0, scalar2=128.0, op0=ALU.mult, op1=ALU.add)
 
         def small(dtype, name):
             return const.tile([P, PLANES], dtype, name=name)
@@ -95,16 +97,23 @@ def tile_dlrkernel_kernel(tc, W, Lambda_im, L, out):
             ml = small(F32, "ml" + label)
             nc.vector.scalar_tensor_tensor(out=ml[:], in0=lam, scalar=k * C2, in1=e1[:], op0=ALU.mult, op1=ALU.add)
             mm = small(I32, "mm" + label)
-            nc.vector.tensor_single_scalar(out=mm[:], in_=mi[:], scalar=TURN_MASK, op=ALU.bitwise_and)
+            nc.vector.tensor_scalar(
+                out=mm[:],
+                in0=mi[:],
+                scalar1=TURN_SHIFT,
+                scalar2=TURN_SHIFT,
+                op0=ALU.logical_shift_left,
+                op1=ALU.arith_shift_right,
+            )
             mh = small(F32, "mh" + label)
             nc.vector.tensor_copy(out=mh[:], in_=mm[:])
             return mi, mh, ml
 
-        mi4, mh4, ml4 = frequency(4.0, "4")
+        mi2, mh2, ml2 = frequency(2.0, "2")
         mi1, mh1, ml1 = frequency(1.0, "1")
         ee = small(I32, "ee")
         nc.vector.tensor_scalar(
-            out=ee[:], in0=mi4[:], scalar1=6, scalar2=TURN_MASK, op0=ALU.logical_shift_left, op1=ALU.bitwise_and
+            out=ee[:], in0=mi2[:], scalar1=7, scalar2=TURN_MASK, op0=ALU.logical_shift_left, op1=ALU.bitwise_and
         )
         ef = small(F32, "ef")
         nc.vector.tensor_copy(out=ef[:], in_=ee[:])
@@ -142,13 +151,13 @@ def tile_dlrkernel_kernel(tc, W, Lambda_im, L, out):
 
             pq = outer(ef, odq, 4, "pq")
             pr = outer(mh1, rho, 3, "pr")
-            lq = outer(ml4, odq64, 4, "lq")
+            lq = outer(ml2, odq128, 4, "lq")
             lr = outer(ml1, rho, 3, "lr")
             pa = cross(pq, pr, "pa")
             la = cross(lq, lr, "la")
             v1a = pool.tile(shape4, I32, name="v1a" + label)
             nc.vector.scalar_tensor_tensor(
-                out=flat(v1a[:]), in0=flat(pa[:]), scalar=U, in1=flat(la[:]), op0=ALU.add, op1=ALU.add
+                out=flat(v1a[:]), in0=flat(pa[:]), scalar=5.0 * U, in1=flat(la[:]), op0=ALU.add, op1=ALU.add
             )
             kua = pool.tile(shape4, I32, name="kua" + label)
             nc.vector.tensor_single_scalar(
@@ -161,34 +170,64 @@ def tile_dlrkernel_kernel(tc, W, Lambda_im, L, out):
             nc.vector.tensor_scalar(
                 out=flat(sc[:, p0:p1]), in0=flat(pba[:]), scalar1=-2.0 * PI_U / U, scalar2=PI_U, op0=ALU.mult, op1=ALU.add
             )
-            nc.vector.tensor_tensor(out=flat(pa[:]), in0=flat(dd[:]), in1=flat(la[:]), op=ALU.add)
+            nc.vector.scalar_tensor_tensor(
+                out=flat(pa[:]), in0=flat(dd[:]), scalar=4.0 * U, in1=flat(la[:]), op0=ALU.add, op1=ALU.add
+            )
             nc.vector.tensor_tensor(out=flat(bi[:, p0:p1]), in0=flat(pa[:]), in1=flat(sc[:, p0:p1]), op=ALU.mult)
 
         t_tab = const.tile([P, PLANES, B], F32, name="t_tab")
         s_tab = const.tile([P, PASSES, B, 4], BF16, name="s_tab")
 
-        def build_tables(c):
-            tmp = early["tmp"]
-            v1 = tmp.tile([P, 4, B], I32, name="v1")
+        v1s = {}
+        ffs = {}
+
+        def halves(tab):
+            return tab.rearrange("p j (m h i) -> p j m h i", m=2, h=2)
+
+        def products(c):
+            v1 = early["tmp"].tile([P, 4, HALF], I32, name="v1")
+            v1s[c] = v1
             for j in range(4):
                 pl = 4 * c + j
                 nc.vector.tensor_scalar(
-                    out=v1[:, j, :], in0=x[:], scalar1=mh4[:, pl : pl + 1], scalar2=U / 2.0, op0=ALU.mult, op1=ALU.add
+                    out=v1[:, j, :], in0=x[:], scalar1=mh2[:, pl : pl + 1], scalar2=U / 2.0, op0=ALU.mult, op1=ALU.add
                 )
-            ff = tmp.tile([P, 4, B], I32, name="ff")
-            nc.vector.tensor_single_scalar(out=ff[:], in_=v1[:], scalar=U_INT - 1, op=ALU.bitwise_and)
-            pb = tmp.tile([P, 4, B], I32, name="pb")
-            nc.vector.tensor_single_scalar(out=pb[:], in_=v1[:], scalar=U_INT, op=ALU.bitwise_and)
+
+        def split(c):
+            ff = early["tmp"].tile([P, 4, HALF], I32, name="ff")
+            nc.vector.tensor_single_scalar(out=ff[:], in_=v1s[c][:], scalar=U_INT - 1, op=ALU.bitwise_and)
+            pb = early["tmp"].tile([P, 4, HALF], I32, name="pb")
+            nc.vector.tensor_single_scalar(out=pb[:], in_=v1s[c][:], scalar=U_INT, op=ALU.bitwise_and)
+            ffs[c] = (ff, pb)
+
+        def upper_half(c):
+            ff, pb = ffs[c]
             for j in range(4):
                 pl = 4 * c + j
                 nc.vector.scalar_tensor_tensor(
-                    out=t_tab[:, pl, :], in0=x[:], scalar=ml4[:, pl : pl + 1], in1=ff[:, j, :], op0=ALU.mult, op1=ALU.add
+                    out=halves(t_tab[:, pl : pl + 1, :])[:, 0, :, 1, :],
+                    in0=x[:].rearrange("p (m i) -> p m i", m=2),
+                    scalar=ml2[:, pl : pl + 1],
+                    in1=ff[:, j, :].rearrange("p (m i) -> p m i", m=2),
+                    op0=ALU.mult,
+                    op1=ALU.add,
                 )
+            st = s_tab[:, c, :, :].rearrange("p (m h i) j -> p m h i j", m=2, h=2)
+            pm = pb[:].rearrange("p j (m i) -> p m i j", m=2)
             nc.vector.tensor_scalar(
-                out=s_tab[:, c, :, :],
-                in0=pb[:].rearrange("p j b -> p b j"),
-                scalar1=-2.0 / U,
-                scalar2=1.0,
+                out=st[:, :, 1, :, :], in0=pm, scalar1=-2.0 / U, scalar2=1.0, op0=ALU.mult, op1=ALU.add
+            )
+            nc.vector.tensor_scalar(
+                out=st[:, :, 0, :, :], in0=pm[:, ::-1, ::-1, :], scalar1=-2.0 / U, scalar2=1.0, op0=ALU.mult, op1=ALU.add
+            )
+
+        def lower_half(c):
+            tv = halves(t_tab[:, 4 * c : 4 * c + 4, :])
+            nc.vector.tensor_scalar(
+                out=tv[:, :, :, 0, :],
+                in0=tv[:, :, ::-1, 1, ::-1],
+                scalar1=-1.0,
+                scalar2=U,
                 op0=ALU.mult,
                 op1=ALU.add,
             )
@@ -219,6 +258,7 @@ def tile_dlrkernel_kernel(tc, W, Lambda_im, L, out):
                 in_=wgs[g][:].rearrange("p h u -> p (h u)").bitcast(BF16),
             )
 
+        e_first = const.tile([P, PLANES, 2, B], F32, name="e_first")
         z_keep = []
         for q in range(2):
             zk = const.tile([P, PLANES, 2, B], F32, name="z_keep%d" % q)
@@ -252,21 +292,19 @@ def tile_dlrkernel_kernel(tc, W, Lambda_im, L, out):
         def sines(u):
             q, c = units[u]
             pls = slice(4 * c, 4 * c + 4)
-            if q != 1 or len(share(u)) > 0:
+            if q >= 2 or len(share(u)) > 0:
                 zh = zpool.tile([P, 8 * B], BF16, name="zh", align_bytes=64)
-            if q != 1:
-                zf = zpool.tile([P, 4, 2, B], F32, name="zf")
             if len(share(u)) > 0:
                 ahead[u] = zh[:].rearrange("p (r b t) -> p r b t", r=2, t=4)
             if q == 0:
                 zo = z_keep[0][:, pls, :, :]
-                z0, z2 = zh[:].rearrange("p (j s b) -> p j s b", j=4, s=2)[:, :, 0:1, :], zf[:, :, 0:1, :]
+                z0, z2 = e_first[:, pls, 0:1, :], e_first[:, pls, 1:2, :]
             elif q == 1:
                 zo = z_keep[1][:, pls, :, :]
                 z0, z2 = late["e_keep"][:, pls, 0:1, :], late["e_keep"][:, pls, 1:2, :]
             else:
                 zo = zh[:].rearrange("p (j s b) -> p j s b", j=4, s=2)
-                z0, z2 = zf[:, :, 0:1, :], zf[:, :, 1:2, :]
+                z0, z2 = z_keep[0][:, pls, 0:1, :], z_keep[0][:, pls, 1:2, :]
             zs[u] = (z0, zo, z2)
             for j in range(4):
                 for s in range(2):
@@ -277,18 +315,21 @@ def tile_dlrkernel_kernel(tc, W, Lambda_im, L, out):
                 func=ACT.Square,
                 scale=math.sqrt(2.0),
             )
-            if q < 2:
+            dst = z0[:, :, 0, :].rearrange("p j (s i m) -> p j s i m", s=2, m=2)
+            if q == 0:
                 for j in range(4):
                     sine(z0[:, j, 0, :], 4 * c + j, q, 0)
-                for r in reversed(share(u)):
-                    regroup_block(u, r, True)
-            else:
-                src = halved(late["e_keep"][:, pls, :, :], q)
-                dst = z0[:, :, 0, :].rearrange("p j (s i m) -> p j s i m", s=2, m=2)
+            elif q == 1:
+                src = halved(e_first[:, pls, :, :], q)
                 nc.scalar.activation(out=dst[:, :, 0:1], in_=src[:, :, 0:1], func=ACT.Square, scale=math.sqrt(2.0))
                 nc.scalar.activation(
                     out=dst[:, :, 1:2], in_=src[:, :, 1:2], func=ACT.Square, scale=math.sqrt(2.0), bias=neg_root2[:]
                 )
+            else:
+                src = halved(late["e_keep"][:, pls, :, :], q)
+                nc.scalar.activation(out=dst, in_=src, func=ACT.Square, scale=math.sqrt(2.0), bias=neg_root2[:])
+            for r in reversed(share(u)):
+                regroup_block(u, r, True)
 
         def block(u, r):
             if r in share(u):
@@ -303,7 +344,7 @@ def tile_dlrkernel_kernel(tc, W, Lambda_im, L, out):
                 src = z2[:, :, 0, :].rearrange("p t (c i) -> p c t i", i=4)
             else:
                 src = zo[:, :, r // 2, :].rearrange("p t (c i) -> p c t i", i=4)
-            if r == 2 or (r == 0 and units[u][0] >= 2):
+            if r == 2 or (r == 0 and units[u][0] >= 1):
                 if on_scalar:
                     nc.scalar.add(block(u, r), src, -1.0)
                 else:
@@ -327,12 +368,14 @@ def tile_dlrkernel_kernel(tc, W, Lambda_im, L, out):
             q, c = units[u]
             st = s_tab[:, c, :, :].rearrange("p b t -> p (b t)")
             two = st.unsqueeze(1).to_broadcast([P, 2, 4 * B])
-            if q < 2:
-                if len(share(u)) > 0:
-                    g01 = ahead[u].rearrange("p r b t -> p r (b t)")
-                else:
-                    g01 = gs[u][:, 0 : 2 * B, :].rearrange("p (r b) t -> p r (b t)", r=2)
+            if q == 0:
+                g01 = gs[u][:, 0 : 2 * B, :].rearrange("p (r b) t -> p r (b t)", r=2)
                 nc.vector.tensor_tensor(out=g01, in0=g01, in1=two, op=ALU.mult)
+                g3 = gs[u][:, 3 * B : 4 * B, :].rearrange("p b t -> p (b t)")
+                nc.vector.tensor_tensor(out=g3, in0=g3, in1=st, op=ALU.mult)
+            elif len(share(u)) > 0:
+                g1 = ahead[u][:, 1, :, :].rearrange("p b t -> p (b t)")
+                nc.vector.tensor_tensor(out=g1, in0=g1, in1=st, op=ALU.mult)
                 g3 = gs[u][:, 3 * B : 4 * B, :].rearrange("p b t -> p (b t)")
                 nc.vector.tensor_tensor(out=g3, in0=g3, in1=st, op=ALU.mult)
             else:
@@ -411,20 +454,21 @@ def tile_dlrkernel_kernel(tc, W, Lambda_im, L, out):
             early["wload"] = first.enter_context(tc.tile_pool(name="wload", bufs=3))
             early["wstage"] = first.enter_context(tc.tile_pool(name="wstage", bufs=3))
             load_w()
+            products(0)
             phases(0, 8, "0")
-            build_tables(0)
-            transpose_w(0)
-            sines(0)
-            build_tables(1)
-            transpose_w(1)
-            sines(1)
-            phases(8, PLANES, "1")
-            for c in range(2, PASSES):
-                build_tables(c)
+            for c in range(PASSES):
+                split(c)
+                if c + 1 < PASSES:
+                    products(c + 1)
+                upper_half(c)
+                if c >= 2:
+                    quantise_w(c - 2)
+                lower_half(c)
+                if c == 1:
+                    phases(8, PLANES, "1")
                 transpose_w(c)
                 if c < LEAD:
                     sines(c)
-                quantise_w(c - 2)
             quantise_w(PASSES - 2)
             quantise_w(PASSES - 1)
         with tc.tile_pool(name="ekeep", bufs=1) as ekeep:

@@ -35,7 +35,6 @@ C2 = C_ALL - C1
 PI_U = math.pi / U
 
 A_CLASSES = (0, 1, 3)
-S_UNITS = ()
 V_BANKS = ((3, 1), (3, 3))
 LEAD = 6
 
@@ -45,7 +44,6 @@ def tile_dlrkernel_kernel(tc, W, Lambda_im, L, out):
     assert L == L_COLS
     with ExitStack() as ctx:
         const = ctx.enter_context(tc.tile_pool(name="const", bufs=1))
-        zpool = ctx.enter_context(tc.tile_pool(name="zpool", bufs=LEAD + 1))
         gpool = ctx.enter_context(tc.tile_pool(name="gpool", bufs=3))
         qpool = ctx.enter_context(tc.tile_pool(name="qpool", bufs=4))
         opool = ctx.enter_context(tc.tile_pool(name="opool", bufs=3))
@@ -268,12 +266,6 @@ def tile_dlrkernel_kernel(tc, W, Lambda_im, L, out):
         acc = {}
         zs = {}
         gs = {}
-        ahead = {}
-
-        def share(u):
-            if units[u] in S_UNITS:
-                return (0, 1)
-            return ()
 
         def sine(dst, pl, q, r):
             k = A_CLASSES.index(r)
@@ -292,20 +284,17 @@ def tile_dlrkernel_kernel(tc, W, Lambda_im, L, out):
         def sines(u):
             q, c = units[u]
             pls = slice(4 * c, 4 * c + 4)
-            if q >= 2 or len(share(u)) > 0:
-                zh = zpool.tile([P, 8 * B], BF16, name="zh", align_bytes=64)
-            if len(share(u)) > 0:
-                ahead[u] = zh[:].rearrange("p (r b t) -> p r b t", r=2, t=4)
             if q == 0:
                 zo = z_keep[0][:, pls, :, :]
-                z0, z2 = e_first[:, pls, 0:1, :], e_first[:, pls, 1:2, :]
+                ze = e_first[:, pls, :, :]
             elif q == 1:
                 zo = z_keep[1][:, pls, :, :]
-                z0, z2 = late["e_keep"][:, pls, 0:1, :], late["e_keep"][:, pls, 1:2, :]
+                ze = late["e_keep"][:, pls, :, :]
             else:
-                zo = zh[:].rearrange("p (j s b) -> p j s b", j=4, s=2)
-                z0, z2 = z_keep[0][:, pls, 0:1, :], z_keep[0][:, pls, 1:2, :]
-            zs[u] = (z0, zo, z2)
+                zo = e_first[:, pls, :, :]
+                ze = z_keep[0][:, pls, :, :]
+            zs[u] = (ze, zo)
+            z0, z2 = ze[:, :, 0:1, :], ze[:, :, 1:2, :]
             for j in range(4):
                 for s in range(2):
                     sine(zo[:, j, s, :], 4 * c + j, q, 1 + 2 * s)
@@ -328,81 +317,47 @@ def tile_dlrkernel_kernel(tc, W, Lambda_im, L, out):
             else:
                 src = halved(late["e_keep"][:, pls, :, :], q)
                 nc.scalar.activation(out=dst, in_=src, func=ACT.Square, scale=math.sqrt(2.0), bias=neg_root2[:])
-            for r in reversed(share(u)):
-                regroup_block(u, r, True)
 
-        def block(u, r):
-            if r in share(u):
-                return ahead[u][:, r, :, :].rearrange("p (c i) t -> p c t i", i=4)
-            return gs[u][:, r * B : (r + 1) * B, :].rearrange("p (c i) t -> p c t i", i=4)
+        def grouped_columns(u, first, count):
+            return gs[u][:, first * B : (first + count) * B, :].rearrange("p (c i) t -> p c t i", i=4)
 
-        def regroup_block(u, r, on_scalar):
-            z0, zo, z2 = zs[u]
-            if r == 0:
-                src = z0[:, :, 0, :].rearrange("p t (c i) -> p c t i", i=4)
-            elif r == 2:
-                src = z2[:, :, 0, :].rearrange("p t (c i) -> p c t i", i=4)
-            else:
-                src = zo[:, :, r // 2, :].rearrange("p t (c i) -> p c t i", i=4)
-            if r == 2 or (r == 0 and units[u][0] >= 1):
-                if on_scalar:
-                    nc.scalar.add(block(u, r), src, -1.0)
-                else:
-                    nc.vector.tensor_scalar(out=block(u, r), in0=src, scalar1=-1.0, scalar2=None, op0=ALU.add)
-            else:
-                if on_scalar:
-                    nc.scalar.copy(out=block(u, r), in_=src)
-                else:
-                    nc.vector.tensor_copy(out=block(u, r), in_=src)
+        def fours(z):
+            return z.rearrange("p t s (c i) -> p (s c) t i", i=4)
 
-        def regroup_scalar(u):
+        def regroup(u):
             grouped = gpool.tile([P, 512, 4], BF16, name="grouped", align_bytes=64)
             gs[u] = grouped
-
-        def regroup_vector(u):
-            for r in (1, 3, 0, 2):
-                if r not in share(u):
-                    regroup_block(u, r, False)
+            ze, zo = zs[u]
+            nc.vector.tensor_copy(out=grouped_columns(u, 2, 2), in_=fours(zo))
+            if units[u][0] == 0:
+                nc.vector.tensor_copy(out=grouped_columns(u, 0, 1), in_=fours(ze[:, :, 0:1, :]))
+                nc.vector.tensor_scalar(
+                    out=grouped_columns(u, 1, 1), in0=fours(ze[:, :, 1:2, :]), scalar1=-1.0, scalar2=None, op0=ALU.add
+                )
+            else:
+                nc.vector.tensor_scalar(
+                    out=grouped_columns(u, 0, 2), in0=fours(ze), scalar1=-1.0, scalar2=None, op0=ALU.add
+                )
 
         def signs(u):
             q, c = units[u]
             st = s_tab[:, c, :, :].rearrange("p b t -> p (b t)")
             two = st.unsqueeze(1).to_broadcast([P, 2, 4 * B])
+            odd = gs[u][:, 2 * B : 4 * B, :].rearrange("p (r b) t -> p r (b t)", r=2)
+            nc.vector.tensor_tensor(out=odd, in0=odd, in1=two, op=ALU.mult)
             if q == 0:
-                g01 = gs[u][:, 0 : 2 * B, :].rearrange("p (r b) t -> p r (b t)", r=2)
-                nc.vector.tensor_tensor(out=g01, in0=g01, in1=two, op=ALU.mult)
-                g3 = gs[u][:, 3 * B : 4 * B, :].rearrange("p b t -> p (b t)")
-                nc.vector.tensor_tensor(out=g3, in0=g3, in1=st, op=ALU.mult)
-            elif len(share(u)) > 0:
-                g1 = ahead[u][:, 1, :, :].rearrange("p b t -> p (b t)")
-                nc.vector.tensor_tensor(out=g1, in0=g1, in1=st, op=ALU.mult)
-                g3 = gs[u][:, 3 * B : 4 * B, :].rearrange("p b t -> p (b t)")
-                nc.vector.tensor_tensor(out=g3, in0=g3, in1=st, op=ALU.mult)
-            else:
-                g13 = gs[u][:].rearrange("p (k r b) t -> p k r (b t)", k=2, r=2)[:, :, 1, :]
-                nc.vector.tensor_tensor(out=g13, in0=g13, in1=two, op=ALU.mult)
+                g0 = gs[u][:, 0:B, :].rearrange("p b t -> p (b t)")
+                nc.vector.tensor_tensor(out=g0, in0=g0, in1=st, op=ALU.mult)
 
         def quantise_and_multiply(u):
             q, c = units[u]
             s_codes = qpool.tile([P, 512], U32, name="s_codes", align_bytes=64)
             s_scales = qpool.tile([P, 512], U8, name="s_scales", align_bytes=64)
-            if len(share(u)) > 0:
-                nc.vector.quantize_mx(
-                    out=s_codes[:, 0 : 2 * B].bitcast(FP8X4),
-                    scales=s_scales[:, 0 : 2 * B],
-                    in_=ahead[u].rearrange("p r b t -> p (r b t)"),
-                )
-                nc.vector.quantize_mx(
-                    out=s_codes[:, 2 * B : 4 * B].bitcast(FP8X4),
-                    scales=s_scales[:, 2 * B : 4 * B],
-                    in_=gs[u][:, 2 * B : 4 * B, :].rearrange("p l t -> p (l t)"),
-                )
-            else:
-                nc.vector.quantize_mx(
-                    out=s_codes[:].bitcast(FP8X4),
-                    scales=s_scales[:],
-                    in_=gs[u][:].rearrange("p l t -> p (l t)"),
-                )
+            nc.vector.quantize_mx(
+                out=s_codes[:].bitcast(FP8X4),
+                scales=s_scales[:],
+                in_=gs[u][:].rearrange("p l t -> p (l t)"),
+            )
             if c == 0:
                 for m in range(4):
                     acc_m = psum.tile([P, 512], F32, name="acc", tag="bank%d" % (4 * (q % 2) + m))
@@ -420,8 +375,8 @@ def tile_dlrkernel_kernel(tc, W, Lambda_im, L, out):
 
         def empty_bank(q, m, on_vector):
             o_sb = opool.tile([P, 512], F32, name="o_sb")
-            dst = o_sb[:].rearrange("p (i s r) -> p i s r", s=2, r=4)
-            src = acc[(q, m)][:].rearrange("p (r s i) -> p i s r", r=4, s=2)
+            dst = o_sb[:].rearrange("p (i s e o) -> p i s e o", s=2, e=2, o=2)
+            src = acc[(q, m)][:].rearrange("p (o e s i) -> p i s e o", o=2, e=2, s=2)
             if on_vector:
                 nc.vector.tensor_copy(out=dst, in_=src)
             else:
@@ -435,8 +390,7 @@ def tile_dlrkernel_kernel(tc, W, Lambda_im, L, out):
         def iteration(u):
             if u + LEAD < n_units:
                 sines(u + LEAD)
-            regroup_scalar(u)
-            regroup_vector(u)
+            regroup(u)
             if u >= 1:
                 quantise_and_multiply(u - 1)
                 q1, c1 = units[u - 1]

@@ -36,6 +36,7 @@ PI_U = math.pi / U
 
 A_CLASSES = (0, 1, 3)
 V_BANKS = ((3, 1), (3, 3))
+W_AHEAD = 3
 LEAD = 6
 
 
@@ -87,28 +88,41 @@ def tile_dlrkernel_kernel(tc, W, Lambda_im, L, out):
 
         lam = lam_bf[:].rearrange("p r e -> p (r e)")
 
+        def weave(first, second):
+            for k in range(max(len(first), len(second))):
+                for steps in (first, second):
+                    if k < len(steps):
+                        steps[k]()
+
         def frequency(k, label):
             mi = small(I32, "mi" + label)
-            nc.vector.tensor_scalar(out=mi[:], in0=lam, scalar1=k * C_ALL, scalar2=None, op0=ALU.mult)
             e1 = small(F32, "e1" + label)
-            nc.vector.scalar_tensor_tensor(out=e1[:], in0=lam, scalar=k * C1, in1=mi[:], op0=ALU.mult, op1=ALU.subtract)
             ml = small(F32, "ml" + label)
-            nc.vector.scalar_tensor_tensor(out=ml[:], in0=lam, scalar=k * C2, in1=e1[:], op0=ALU.mult, op1=ALU.add)
             mm = small(I32, "mm" + label)
-            nc.vector.tensor_scalar(
-                out=mm[:],
-                in0=mi[:],
-                scalar1=TURN_SHIFT,
-                scalar2=TURN_SHIFT,
-                op0=ALU.logical_shift_left,
-                op1=ALU.arith_shift_right,
-            )
             mh = small(F32, "mh" + label)
-            nc.vector.tensor_copy(out=mh[:], in_=mm[:])
-            return mi, mh, ml
+            steps = [
+                lambda: nc.vector.tensor_scalar(out=mi[:], in0=lam, scalar1=k * C_ALL, scalar2=None, op0=ALU.mult),
+                lambda: nc.vector.tensor_scalar(
+                    out=mm[:],
+                    in0=mi[:],
+                    scalar1=TURN_SHIFT,
+                    scalar2=TURN_SHIFT,
+                    op0=ALU.logical_shift_left,
+                    op1=ALU.arith_shift_right,
+                ),
+                lambda: nc.vector.scalar_tensor_tensor(
+                    out=e1[:], in0=lam, scalar=k * C1, in1=mi[:], op0=ALU.mult, op1=ALU.subtract
+                ),
+                lambda: nc.vector.tensor_copy(out=mh[:], in_=mm[:]),
+                lambda: nc.vector.scalar_tensor_tensor(
+                    out=ml[:], in0=lam, scalar=k * C2, in1=e1[:], op0=ALU.mult, op1=ALU.add
+                ),
+            ]
+            return mi, mh, ml, steps
 
-        mi2, mh2, ml2 = frequency(2.0, "2")
-        mi1, mh1, ml1 = frequency(1.0, "1")
+        mi2, mh2, ml2, steps2 = frequency(2.0, "2")
+        mi1, mh1, ml1, steps1 = frequency(1.0, "1")
+        weave(steps2, steps1)
         ee = small(I32, "ee")
         nc.vector.tensor_scalar(
             out=ee[:], in0=mi2[:], scalar1=7, scalar2=TURN_MASK, op0=ALU.logical_shift_left, op1=ALU.bitwise_and
@@ -123,61 +137,73 @@ def tile_dlrkernel_kernel(tc, W, Lambda_im, L, out):
             shape4 = [P, p1 - p0, 4, 3]
             pool = early["ph"]
 
-            def outer(v, tab, width, name):
-                shape2 = [P, p1 - p0, width]
-                o = pool.tile(shape2, F32, name=name + label)
+            def tile4(dtype, name):
+                return pool.tile(shape4, dtype, name=name + label)
+
+            def flat(t):
+                return t.rearrange("p a q r -> p (a q r)")
+
+            def outer(o, v, tab):
+                shape2 = list(o.shape)
                 nc.vector.tensor_tensor(
                     out=o[:],
                     in0=v[:, p0:p1].unsqueeze(2).to_broadcast(shape2),
                     in1=tab[:].unsqueeze(1).to_broadcast(shape2),
                     op=ALU.mult,
                 )
-                return o
 
-            def cross(a, b, name):
-                o = pool.tile(shape4, F32, name=name + label)
+            def cross(o, a, b):
                 nc.vector.tensor_tensor(
                     out=o[:],
                     in0=a[:].unsqueeze(3).to_broadcast(shape4),
                     in1=b[:].unsqueeze(2).to_broadcast(shape4),
                     op=ALU.add,
                 )
-                return o
 
-            def flat(t):
-                return t.rearrange("p a q r -> p (a q r)")
-
-            pq = outer(ef, odq, 4, "pq")
-            pr = outer(mh1, rho, 3, "pr")
-            lq = outer(ml2, odq128, 4, "lq")
-            lr = outer(ml1, rho, 3, "lr")
-            pa = cross(pq, pr, "pa")
-            la = cross(lq, lr, "la")
-            v1a = pool.tile(shape4, I32, name="v1a" + label)
-            nc.vector.scalar_tensor_tensor(
-                out=flat(v1a[:]), in0=flat(pa[:]), scalar=5.0 * U, in1=flat(la[:]), op0=ALU.add, op1=ALU.add
-            )
-            kua = pool.tile(shape4, I32, name="kua" + label)
-            nc.vector.tensor_single_scalar(
-                out=flat(kua[:]), in_=flat(v1a[:]), scalar=0xFFFFFF - (U_INT - 1), op=ALU.bitwise_and
-            )
-            pba = pool.tile(shape4, I32, name="pba" + label)
-            nc.vector.tensor_single_scalar(out=flat(pba[:]), in_=flat(v1a[:]), scalar=U_INT, op=ALU.bitwise_and)
-            dd = pool.tile(shape4, F32, name="dd" + label)
-            nc.vector.tensor_tensor(out=flat(dd[:]), in0=flat(pa[:]), in1=flat(kua[:]), op=ALU.subtract)
-            nc.vector.tensor_scalar(
-                out=flat(sc[:, p0:p1]), in0=flat(pba[:]), scalar1=-2.0 * PI_U / U, scalar2=PI_U, op0=ALU.mult, op1=ALU.add
-            )
-            nc.vector.scalar_tensor_tensor(
-                out=flat(pa[:]), in0=flat(dd[:]), scalar=4.0 * U, in1=flat(la[:]), op0=ALU.add, op1=ALU.add
-            )
-            nc.vector.tensor_tensor(out=flat(bi[:, p0:p1]), in0=flat(pa[:]), in1=flat(sc[:, p0:p1]), op=ALU.mult)
+            pq = pool.tile([P, p1 - p0, 4], F32, name="pq" + label)
+            pr = pool.tile([P, p1 - p0, 3], F32, name="pr" + label)
+            lq = pool.tile([P, p1 - p0, 4], F32, name="lq" + label)
+            lr = pool.tile([P, p1 - p0, 3], F32, name="lr" + label)
+            pa = tile4(F32, "pa")
+            la = tile4(F32, "la")
+            v1a = tile4(I32, "v1a")
+            kua = tile4(I32, "kua")
+            pba = tile4(I32, "pba")
+            dd = tile4(F32, "dd")
+            db = tile4(F32, "db")
+            sc_p = flat(sc[:, p0:p1])
+            return [
+                lambda: outer(lq, ml2, odq128),
+                lambda: outer(lr, ml1, rho),
+                lambda: outer(pr, mh1, rho),
+                lambda: outer(pq, ef, odq),
+                lambda: cross(la, lq, lr),
+                lambda: cross(pa, pq, pr),
+                lambda: nc.vector.scalar_tensor_tensor(
+                    out=flat(v1a[:]), in0=flat(pa[:]), scalar=5.0 * U, in1=flat(la[:]), op0=ALU.add, op1=ALU.add
+                ),
+                lambda: nc.vector.tensor_single_scalar(
+                    out=flat(kua[:]), in_=flat(v1a[:]), scalar=0xFFFFFF - (U_INT - 1), op=ALU.bitwise_and
+                ),
+                lambda: nc.vector.tensor_single_scalar(
+                    out=flat(pba[:]), in_=flat(v1a[:]), scalar=U_INT, op=ALU.bitwise_and
+                ),
+                lambda: nc.vector.tensor_tensor(
+                    out=flat(dd[:]), in0=flat(pa[:]), in1=flat(kua[:]), op=ALU.subtract
+                ),
+                lambda: nc.vector.tensor_scalar(
+                    out=sc_p, in0=flat(pba[:]), scalar1=-2.0 * PI_U / U, scalar2=PI_U, op0=ALU.mult, op1=ALU.add
+                ),
+                lambda: nc.vector.scalar_tensor_tensor(
+                    out=flat(db[:]), in0=flat(dd[:]), scalar=4.0 * U, in1=flat(la[:]), op0=ALU.add, op1=ALU.add
+                ),
+                lambda: nc.vector.tensor_tensor(out=flat(bi[:, p0:p1]), in0=flat(db[:]), in1=sc_p, op=ALU.mult),
+            ]
 
         t_tab = const.tile([P, PLANES, B], F32, name="t_tab")
         s_tab = const.tile([P, PASSES, B, 4], BF16, name="s_tab")
 
         v1s = {}
-        ffs = {}
 
         def halves(tab):
             return tab.rearrange("p j (m h i) -> p j m h i", m=2, h=2)
@@ -185,22 +211,21 @@ def tile_dlrkernel_kernel(tc, W, Lambda_im, L, out):
         def products(c):
             v1 = early["tmp"].tile([P, 4, HALF], I32, name="v1")
             v1s[c] = v1
-            for j in range(4):
+
+            def product(j):
                 pl = 4 * c + j
                 nc.vector.tensor_scalar(
                     out=v1[:, j, :], in0=x[:], scalar1=mh2[:, pl : pl + 1], scalar2=U / 2.0, op0=ALU.mult, op1=ALU.add
                 )
 
-        def split(c):
-            ff = early["tmp"].tile([P, 4, HALF], I32, name="ff")
-            nc.vector.tensor_single_scalar(out=ff[:], in_=v1s[c][:], scalar=U_INT - 1, op=ALU.bitwise_and)
-            pb = early["tmp"].tile([P, 4, HALF], I32, name="pb")
-            nc.vector.tensor_single_scalar(out=pb[:], in_=v1s[c][:], scalar=U_INT, op=ALU.bitwise_and)
-            ffs[c] = (ff, pb)
+            return [lambda j=j: product(j) for j in range(4)]
 
-        def upper_half(c):
-            ff, pb = ffs[c]
-            for j in range(4):
+        def table(c):
+            ff = early["tmp"].tile([P, 4, HALF], I32, name="ff")
+            pb = early["tmp"].tile([P, 4, HALF], I32, name="pb")
+            v1 = v1s[c]
+
+            def upper(j):
                 pl = 4 * c + j
                 nc.vector.scalar_tensor_tensor(
                     out=halves(t_tab[:, pl : pl + 1, :])[:, 0, :, 1, :],
@@ -210,24 +235,36 @@ def tile_dlrkernel_kernel(tc, W, Lambda_im, L, out):
                     op0=ALU.mult,
                     op1=ALU.add,
                 )
+
             st = s_tab[:, c, :, :].rearrange("p (m h i) j -> p m h i j", m=2, h=2)
             pm = pb[:].rearrange("p j (m i) -> p m i j", m=2)
-            nc.vector.tensor_scalar(
-                out=st[:, :, 1, :, :], in0=pm, scalar1=-2.0 / U, scalar2=1.0, op0=ALU.mult, op1=ALU.add
-            )
-            nc.vector.tensor_scalar(
-                out=st[:, :, 0, :, :], in0=pm[:, ::-1, ::-1, :], scalar1=-2.0 / U, scalar2=1.0, op0=ALU.mult, op1=ALU.add
-            )
 
-        def lower_half(c):
-            tv = halves(t_tab[:, 4 * c : 4 * c + 4, :])
-            nc.vector.tensor_scalar(
-                out=tv[:, :, :, 0, :],
-                in0=tv[:, :, ::-1, 1, ::-1],
-                scalar1=-1.0,
-                scalar2=U,
-                op0=ALU.mult,
-                op1=ALU.add,
+            def sign(h, source):
+                nc.vector.tensor_scalar(
+                    out=st[:, :, h, :, :], in0=source, scalar1=-2.0 / U, scalar2=1.0, op0=ALU.mult, op1=ALU.add
+                )
+
+            def lower():
+                tv = halves(t_tab[:, 4 * c : 4 * c + 4, :])
+                nc.vector.tensor_scalar(
+                    out=tv[:, :, :, 0, :],
+                    in0=tv[:, :, ::-1, 1, ::-1],
+                    scalar1=-1.0,
+                    scalar2=U,
+                    op0=ALU.mult,
+                    op1=ALU.add,
+                )
+
+            return (
+                [
+                    lambda: nc.vector.tensor_single_scalar(out=ff[:], in_=v1[:], scalar=U_INT - 1, op=ALU.bitwise_and),
+                    lambda: nc.vector.tensor_single_scalar(out=pb[:], in_=v1[:], scalar=U_INT, op=ALU.bitwise_and),
+                ]
+                + (products(c + 1) if c + 1 < PASSES else [])
+                + [lambda j=j: upper(j) for j in range(4)]
+                + [lambda: sign(1, pm), lambda: sign(0, pm[:, ::-1, ::-1, :])]
+                + ([lambda: quantise_w(c - 2)] if c >= 2 else [])
+                + [lower]
             )
 
         w_codes = const.tile([P, PASSES, H], U32, name="w_codes", align_bytes=64)
@@ -405,24 +442,21 @@ def tile_dlrkernel_kernel(tc, W, Lambda_im, L, out):
         with ExitStack() as first:
             early["tmp"] = first.enter_context(tc.tile_pool(name="tmp", bufs=2))
             early["ph"] = first.enter_context(tc.tile_pool(name="ph", bufs=1))
-            early["wload"] = first.enter_context(tc.tile_pool(name="wload", bufs=3))
-            early["wstage"] = first.enter_context(tc.tile_pool(name="wstage", bufs=3))
+            early["wload"] = first.enter_context(tc.tile_pool(name="wload", bufs=W_AHEAD + 1))
+            early["wstage"] = first.enter_context(tc.tile_pool(name="wstage", bufs=W_AHEAD + 2))
             load_w()
-            products(0)
-            phases(0, 8, "0")
-            for c in range(PASSES):
-                split(c)
-                if c + 1 < PASSES:
-                    products(c + 1)
-                upper_half(c)
-                if c >= 2:
-                    quantise_w(c - 2)
-                lower_half(c)
-                if c == 1:
-                    phases(8, PLANES, "1")
+            for c in range(W_AHEAD):
                 transpose_w(c)
+            for step in products(0):
+                step()
+            weave(table(0), phases(0, 8, "0"))
+            for c in range(PASSES):
+                if c >= 1:
+                    weave(table(c), phases(8, PLANES, "1") if c == 1 else [])
                 if c < LEAD:
                     sines(c)
+                if c + W_AHEAD < PASSES:
+                    transpose_w(c + W_AHEAD)
             quantise_w(PASSES - 2)
             quantise_w(PASSES - 1)
         with tc.tile_pool(name="ekeep", bufs=1) as ekeep:

@@ -35,7 +35,8 @@ C2 = C_ALL - C1
 PI_U = math.pi / U
 
 A_CLASSES = (0, 1, 3)
-V_BANKS = ((3, 1), (3, 3))
+V_BANKS = (0, 1)
+ACC_BANKS = 6
 W_AHEAD = 3
 LEAD = 6
 
@@ -47,7 +48,7 @@ def tile_dlrkernel_kernel(tc, W, Lambda_im, L, out):
         const = ctx.enter_context(tc.tile_pool(name="const", bufs=1))
         gpool = ctx.enter_context(tc.tile_pool(name="gpool", bufs=3))
         qpool = ctx.enter_context(tc.tile_pool(name="qpool", bufs=4))
-        opool = ctx.enter_context(tc.tile_pool(name="opool", bufs=3))
+        opool = ctx.enter_context(tc.tile_pool(name="opool", bufs=6))
         psum = ctx.enter_context(tc.psum_pool(name="psum", bufs=1))
         early = {}
         late = {}
@@ -65,6 +66,8 @@ def tile_dlrkernel_kernel(tc, W, Lambda_im, L, out):
 
         ident = const.tile([P, P], F32, name="ident")
         make_identity(nc, ident[:])
+        ident_bf = const.tile([P, P], BF16, name="ident_bf")
+        make_identity(nc, ident_bf[:])
         xi = const.tile([P, HALF], I32, name="xi")
         nc.gpsimd.iota(xi[:], pattern=[[2, 2], [4, HALF // 2]], base=1, channel_multiplier=0)
         ri = const.tile([P, 4], I32, name="ri")
@@ -303,6 +306,7 @@ def tile_dlrkernel_kernel(tc, W, Lambda_im, L, out):
         acc = {}
         zs = {}
         gs = {}
+        zgs = {}
 
         def sine(dst, pl, q, r):
             k = A_CLASSES.index(r)
@@ -328,7 +332,8 @@ def tile_dlrkernel_kernel(tc, W, Lambda_im, L, out):
                 zo = z_keep[1][:, pls, :, :]
                 ze = late["e_keep"][:, pls, :, :]
             else:
-                zo = e_first[:, pls, :, :]
+                zh = late["zpool"].tile([P, 4, 2, B], BF16, name="zh")
+                zo = zh[:]
                 ze = z_keep[0][:, pls, :, :]
             zs[u] = (ze, zo)
             z0, z2 = ze[:, :, 0:1, :], ze[:, :, 1:2, :]
@@ -365,7 +370,8 @@ def tile_dlrkernel_kernel(tc, W, Lambda_im, L, out):
             grouped = gpool.tile([P, 512, 4], BF16, name="grouped", align_bytes=64)
             gs[u] = grouped
             ze, zo = zs[u]
-            nc.vector.tensor_copy(out=grouped_columns(u, 2, 2), in_=fours(zo))
+            if units[u][0] < 2:
+                nc.vector.tensor_copy(out=grouped_columns(u, 2, 2), in_=fours(zo))
             if units[u][0] == 0:
                 nc.vector.tensor_copy(out=grouped_columns(u, 0, 1), in_=fours(ze[:, :, 0:1, :]))
                 nc.vector.tensor_scalar(
@@ -376,12 +382,25 @@ def tile_dlrkernel_kernel(tc, W, Lambda_im, L, out):
                     out=grouped_columns(u, 0, 2), in0=fours(ze), scalar1=-1.0, scalar2=None, op0=ALU.add
                 )
 
+        def regroup_on_tensor(u):
+            zg = psum.tile([P, 2, 4 * B], BF16, name="zg", tag="bank%d" % (ACC_BANKS + u % 2))
+            zgs[u] = zg
+            zo = zs[u][1]
+            for s in range(2):
+                nc.tensor.matmul(
+                    zg[:, s, :],
+                    lhsT=ident_bf[:],
+                    rhs=zo[:, :, s, :].rearrange("p t b -> p b t"),
+                    start=True,
+                    stop=True,
+                )
+
         def signs(u):
             q, c = units[u]
             st = s_tab[:, c, :, :].rearrange("p b t -> p (b t)")
             two = st.unsqueeze(1).to_broadcast([P, 2, 4 * B])
             odd = gs[u][:, 2 * B : 4 * B, :].rearrange("p (r b) t -> p r (b t)", r=2)
-            nc.vector.tensor_tensor(out=odd, in0=odd, in1=two, op=ALU.mult)
+            nc.vector.tensor_tensor(out=odd, in0=odd if q < 2 else zgs[u][:], in1=two, op=ALU.mult)
             if q == 0:
                 g0 = gs[u][:, 0:B, :].rearrange("p b t -> p (b t)")
                 nc.vector.tensor_tensor(out=g0, in0=g0, in1=st, op=ALU.mult)
@@ -397,7 +416,7 @@ def tile_dlrkernel_kernel(tc, W, Lambda_im, L, out):
             )
             if c == 0:
                 for m in range(4):
-                    acc_m = psum.tile([P, 512], F32, name="acc", tag="bank%d" % (4 * (q % 2) + m))
+                    acc_m = psum.tile([P, 512], F32, name="acc", tag="bank%d" % ((4 * q + m) % ACC_BANKS))
                     acc[(q, m)] = acc_m
             for m in range(4):
                 nc.tensor.matmul_mx(
@@ -421,23 +440,22 @@ def tile_dlrkernel_kernel(tc, W, Lambda_im, L, out):
             nc.sync.dma_start(out=out[0, m * P : (m + 1) * P, 512 * q : 512 * (q + 1)], in_=o_sb[:])
 
         n_units = len(units)
-        to_empty = []
-        emptied = [0]
 
         def iteration(u):
+            q, c = units[u]
             if u + LEAD < n_units:
                 sines(u + LEAD)
             regroup(u)
+            if u + 1 < n_units and units[u + 1][0] >= 2:
+                regroup_on_tensor(u + 1)
             if u >= 1:
                 quantise_and_multiply(u - 1)
-                q1, c1 = units[u - 1]
-                if c1 == PASSES - 1:
-                    to_empty.extend([(q1, m) for m in range(4)])
             signs(u)
-            if len(to_empty) > emptied[0] and units[u][1] >= 1:
-                q0, m0 = to_empty[emptied[0]]
-                emptied[0] = emptied[0] + 1
-                empty_bank(q0, m0, (q0, m0) in V_BANKS)
+            if q >= 1 and c == 0:
+                for m in V_BANKS:
+                    empty_bank(q - 1, m, True)
+            if q >= 1 and c in (1, 2):
+                empty_bank(q - 1, c + 1, False)
 
         with ExitStack() as first:
             early["tmp"] = first.enter_context(tc.tile_pool(name="tmp", bufs=2))
@@ -459,11 +477,12 @@ def tile_dlrkernel_kernel(tc, W, Lambda_im, L, out):
                     transpose_w(c + W_AHEAD)
             quantise_w(PASSES - 2)
             quantise_w(PASSES - 1)
-        with tc.tile_pool(name="ekeep", bufs=1) as ekeep:
+        with tc.tile_pool(name="ekeep", bufs=1) as ekeep, tc.tile_pool(name="zpool", bufs=LEAD + 1) as zpool:
+            late["zpool"] = zpool
             e_keep = ekeep.tile([P, PLANES, 2, B], F32, name="e_keep")
             late["e_keep"] = e_keep
             for u in range(n_units):
                 iteration(u)
             quantise_and_multiply(n_units - 1)
             for m in range(4):
-                empty_bank(ROUNDS - 1, m, (ROUNDS - 1, m) in V_BANKS)
+                empty_bank(ROUNDS - 1, m, m % 2 == 1)

@@ -388,9 +388,9 @@ def tile_dlrkernel_kernel(tc, W, Lambda_im, L, out):
             zo = zs[u][1]
             for s in range(2):
                 nc.tensor.matmul(
-                    zg[:, s, :],
+                    zg[:, s, :].rearrange("p (b t) -> p t b", t=4),
                     lhsT=ident_bf[:],
-                    rhs=zo[:, :, s, :].rearrange("p t b -> p b t"),
+                    rhs=zo[:, :, s, :],
                     start=True,
                     stop=True,
                 )

@@ -35,7 +35,7 @@ C2 = C_ALL - C1
 PI_U = math.pi / U
 
 A_CLASSES = (0, 1, 3)
-V_BANKS = (0, 1)
+URGENT = (0, 1)
 ACC_BANKS = 6
 W_AHEAD = 3
 LEAD = 6
@@ -322,43 +322,53 @@ def tile_dlrkernel_kernel(tc, W, Lambda_im, L, out):
             v = src.rearrange("p j s (m h i) -> p j s m h i", m=2, h=2)
             return v[:, :, :, :, q % 2, :].rearrange("p j s m i -> p j s i m")
 
+        def even_place(q, planes):
+            if q == 0:
+                return e_first[:, planes, :, :]
+            if q == 1:
+                return late["e_keep"][:, planes, :, :]
+            return z_keep[0][:, planes, :, :]
+
+        def squares(q, c0):
+            planes = slice(4 * c0, 4 * c0 + 8)
+            ze = even_place(q, planes)
+
+            def place(k):
+                return ze[:, :, k, :].rearrange("p j (s i m) -> p j s i m", s=2, m=2)
+
+            root2 = math.sqrt(2.0)
+            if q == 1:
+                src = halved(e_first[:, planes, :, :], q)
+                dst = place(0)
+                nc.scalar.activation(out=dst[:, :, 0:1], in_=src[:, :, 0:1], func=ACT.Square, scale=root2)
+                nc.scalar.activation(
+                    out=dst[:, :, 1:2], in_=src[:, :, 1:2], func=ACT.Square, scale=root2, bias=neg_root2[:]
+                )
+            elif q >= 2:
+                src = halved(late["e_keep"][:, planes, :, :], q)
+                nc.scalar.activation(out=place(0), in_=src, func=ACT.Square, scale=root2, bias=neg_root2[:])
+            nc.scalar.activation(
+                out=place(1), in_=halved(z_keep[q // 2][:, planes, :, :], q), func=ACT.Square, scale=root2
+            )
+
         def sines(u):
             q, c = units[u]
-            pls = slice(4 * c, 4 * c + 4)
-            if q == 0:
-                zo = z_keep[0][:, pls, :, :]
-                ze = e_first[:, pls, :, :]
-            elif q == 1:
-                zo = z_keep[1][:, pls, :, :]
-                ze = late["e_keep"][:, pls, :, :]
+            planes = slice(4 * c, 4 * c + 4)
+            if q < 2:
+                zo = z_keep[q][:, planes, :, :]
             else:
                 zh = late["zpool"].tile([P, 4, 2, B], BF16, name="zh")
                 zo = zh[:]
-                ze = z_keep[0][:, pls, :, :]
+            ze = even_place(q, planes)
             zs[u] = (ze, zo)
-            z0, z2 = ze[:, :, 0:1, :], ze[:, :, 1:2, :]
             for j in range(4):
                 for s in range(2):
                     sine(zo[:, j, s, :], 4 * c + j, q, 1 + 2 * s)
-            nc.scalar.activation(
-                out=z2[:, :, 0, :].rearrange("p j (s i m) -> p j s i m", s=2, m=2),
-                in_=halved(z_keep[q // 2][:, pls, :, :], q),
-                func=ACT.Square,
-                scale=math.sqrt(2.0),
-            )
-            dst = z0[:, :, 0, :].rearrange("p j (s i m) -> p j s i m", s=2, m=2)
             if q == 0:
                 for j in range(4):
-                    sine(z0[:, j, 0, :], 4 * c + j, q, 0)
-            elif q == 1:
-                src = halved(e_first[:, pls, :, :], q)
-                nc.scalar.activation(out=dst[:, :, 0:1], in_=src[:, :, 0:1], func=ACT.Square, scale=math.sqrt(2.0))
-                nc.scalar.activation(
-                    out=dst[:, :, 1:2], in_=src[:, :, 1:2], func=ACT.Square, scale=math.sqrt(2.0), bias=neg_root2[:]
-                )
-            else:
-                src = halved(late["e_keep"][:, pls, :, :], q)
-                nc.scalar.activation(out=dst, in_=src, func=ACT.Square, scale=math.sqrt(2.0), bias=neg_root2[:])
+                    sine(ze[:, j, 0, :], 4 * c + j, q, 0)
+            if c % 2 == 1:
+                squares(q, c - 1)
 
         def grouped_columns(u, first, count):
             return gs[u][:, first * B : (first + count) * B, :].rearrange("p (c i) t -> p c t i", i=4)
@@ -452,10 +462,10 @@ def tile_dlrkernel_kernel(tc, W, Lambda_im, L, out):
                 quantise_and_multiply(u - 1)
             signs(u)
             if q >= 1 and c == 0:
-                for m in V_BANKS:
+                for m in URGENT:
                     empty_bank(q - 1, m, True)
             if q >= 1 and c in (1, 2):
-                empty_bank(q - 1, c + 1, False)
+                empty_bank(q - 1, c + 1, q >= 2)
 
         with ExitStack() as first:
             early["tmp"] = first.enter_context(tc.tile_pool(name="tmp", bufs=2))

@@ -61,7 +61,8 @@ def tile_dlrkernel_kernel(tc, W, Lambda_im, L, out):
         def load_w():
             for g in range(PASSES):
                 wld = early["wload"].tile([P, 4, 512], BF16, name="wld")
-                nc.sync.dma_start(out=wld[:], in_=w_view[:, :, 512 * g : 512 * (g + 1)])
+                for m0, m1 in ((0, 2), (2, 4)) if g == 0 else ((0, 4),):
+                    nc.sync.dma_start(out=wld[:, m0:m1, :], in_=w_view[:, m0:m1, 512 * g : 512 * (g + 1)])
                 wlds.append(wld)
 
         ident = const.tile([P, P], F32, name="ident")
@@ -303,6 +304,7 @@ def tile_dlrkernel_kernel(tc, W, Lambda_im, L, out):
             z_keep.append(zk)
 
         units = [(q, c) for q in range(ROUNDS) for c in range(PASSES)]
+        n_units = len(units)
         acc = {}
         zs = {}
         gs = {}
@@ -329,8 +331,8 @@ def tile_dlrkernel_kernel(tc, W, Lambda_im, L, out):
                 return late["e_keep"][:, planes, :, :]
             return z_keep[0][:, planes, :, :]
 
-        def squares(q, c0):
-            planes = slice(4 * c0, 4 * c0 + 8)
+        def squares(q, c0, count):
+            planes = slice(4 * c0, 4 * (c0 + count))
             ze = even_place(q, planes)
 
             def place(k):
@@ -361,14 +363,23 @@ def tile_dlrkernel_kernel(tc, W, Lambda_im, L, out):
                 zo = zh[:]
             ze = even_place(q, planes)
             zs[u] = (ze, zo)
+            alone = u >= n_units - 2
+            if q >= 2 and c % 2 == 0 and not alone:
+                squares(q, c, 2)
             for j in range(4):
                 for s in range(2):
                     sine(zo[:, j, s, :], 4 * c + j, q, 1 + 2 * s)
             if q == 0:
                 for j in range(4):
                     sine(ze[:, j, 0, :], 4 * c + j, q, 0)
-            if c % 2 == 1:
-                squares(q, c - 1)
+            if alone:
+                squares(q, c, 1)
+            elif q < 2 and c % 2 == 1:
+                squares(q, c - 1, 2)
+
+        def on_tensor(u):
+            q, c = units[u]
+            return 0 if q < 2 else 1 + c % 2
 
         def grouped_columns(u, first, count):
             return gs[u][:, first * B : (first + count) * B, :].rearrange("p (c i) t -> p c t i", i=4)
@@ -380,8 +391,9 @@ def tile_dlrkernel_kernel(tc, W, Lambda_im, L, out):
             grouped = gpool.tile([P, 512, 4], BF16, name="grouped", align_bytes=64)
             gs[u] = grouped
             ze, zo = zs[u]
-            if units[u][0] < 2:
-                nc.vector.tensor_copy(out=grouped_columns(u, 2, 2), in_=fours(zo))
+            moved = on_tensor(u)
+            if moved < 2:
+                nc.vector.tensor_copy(out=grouped_columns(u, 2 + moved, 2 - moved), in_=fours(zo[:, :, moved:2, :]))
             if units[u][0] == 0:
                 nc.vector.tensor_copy(out=grouped_columns(u, 0, 1), in_=fours(ze[:, :, 0:1, :]))
                 nc.vector.tensor_scalar(
@@ -393,10 +405,10 @@ def tile_dlrkernel_kernel(tc, W, Lambda_im, L, out):
                 )
 
         def regroup_on_tensor(u):
-            zg = psum.tile([P, 2, 4 * B], BF16, name="zg", tag="bank%d" % (ACC_BANKS + u % 2))
+            zg = psum.tile([P, on_tensor(u), 4 * B], BF16, name="zg", tag="bank%d" % (ACC_BANKS + u % 2))
             zgs[u] = zg
             zo = zs[u][1]
-            for s in range(2):
+            for s in range(on_tensor(u)):
                 nc.tensor.matmul(
                     zg[:, s, :].rearrange("p (b t) -> p t b", t=4),
                     lhsT=ident_bf[:],
@@ -410,7 +422,12 @@ def tile_dlrkernel_kernel(tc, W, Lambda_im, L, out):
             st = s_tab[:, c, :, :].rearrange("p b t -> p (b t)")
             two = st.unsqueeze(1).to_broadcast([P, 2, 4 * B])
             odd = gs[u][:, 2 * B : 4 * B, :].rearrange("p (r b) t -> p r (b t)", r=2)
-            nc.vector.tensor_tensor(out=odd, in0=odd if q < 2 else zgs[u][:], in1=two, op=ALU.mult)
+            moved = on_tensor(u)
+            if moved == 1:
+                nc.vector.tensor_tensor(out=odd[:, 0, :], in0=zgs[u][:, 0, :], in1=st, op=ALU.mult)
+                nc.vector.tensor_tensor(out=odd[:, 1, :], in0=odd[:, 1, :], in1=st, op=ALU.mult)
+            else:
+                nc.vector.tensor_tensor(out=odd, in0=odd if moved == 0 else zgs[u][:], in1=two, op=ALU.mult)
             if q == 0:
                 g0 = gs[u][:, 0:B, :].rearrange("p b t -> p (b t)")
                 nc.vector.tensor_tensor(out=g0, in0=g0, in1=st, op=ALU.mult)
@@ -449,8 +466,6 @@ def tile_dlrkernel_kernel(tc, W, Lambda_im, L, out):
                 nc.scalar.copy(out=dst, in_=src)
             nc.sync.dma_start(out=out[0, m * P : (m + 1) * P, 512 * q : 512 * (q + 1)], in_=o_sb[:])
 
-        n_units = len(units)
-
         def iteration(u):
             q, c = units[u]
             if u + LEAD < n_units:
@@ -465,7 +480,7 @@ def tile_dlrkernel_kernel(tc, W, Lambda_im, L, out):
                 for m in URGENT:
                     empty_bank(q - 1, m, True)
             if q >= 1 and c in (1, 2):
-                empty_bank(q - 1, c + 1, q >= 2)
+                empty_bank(q - 1, c + 1, False)
 
         with ExitStack() as first:
             early["tmp"] = first.enter_context(tc.tile_pool(name="tmp", bufs=2))

import math
from contextlib import ExitStack

import concourse.mybir as mybir
from concourse.masks import make_identity

F32 = mybir.dt.float32
BF16 = mybir.dt.bfloat16
I32 = mybir.dt.int32
U32 = mybir.dt.uint32
U8 = mybir.dt.uint8
FP8X4 = mybir.dt.float8_e4m3fn_x4
ALU = mybir.AluOpType
ACT = mybir.ActivationFunctionType

P = 128
H = 512
N = 4096
L_COLS = 2048
FLOPS = 2 * H * N * L_COLS

PASSES = N // 512
PLANES = 4 * PASSES
B = 128
HALF = B // 2
ROUNDS = 4

U = 131072.0
U_INT = 131072
TURN_MASK = 2 * U_INT - 1
TURN_SHIFT = 14
C_ALL = U / math.pi
C1 = 41722.0
C2 = C_ALL - C1
PI_U = math.pi / U

A_CLASSES = (0, 1, 3)
URGENT = (0, 1)
ACC_BANKS = 6
W_AHEAD = 3
LEAD = 6


def tile_dlrkernel_kernel(tc, W, Lambda_im, L, out):
    nc = tc.nc
    assert L == L_COLS
    with ExitStack() as ctx:
        const = ctx.enter_context(tc.tile_pool(name="const", bufs=1))
        gpool = ctx.enter_context(tc.tile_pool(name="gpool", bufs=3))
        qpool = ctx.enter_context(tc.tile_pool(name="qpool", bufs=4))
        opool = ctx.enter_context(tc.tile_pool(name="opool", bufs=6))
        psum = ctx.enter_context(tc.psum_pool(name="psum", bufs=1))
        early = {}
        late = {}

        lam_bf = const.tile([P, 16, 2], BF16, name="lam_bf")
        nc.sync.dma_start(out=lam_bf[:], in_=Lambda_im.rearrange("(r p e) -> p r e", p=P, e=2))
        w_view = W[0].rearrange("(m p) n -> p m n", p=P)
        wlds = []

        def load_w():
            for g in range(PASSES):
                wld = early["wload"].tile([P, 4, 512], BF16, name="wld")
                for m0, m1 in ((0, 2), (2, 4)) if g == 0 else ((0, 4),):
                    nc.sync.dma_start(out=wld[:, m0:m1, :], in_=w_view[:, m0:m1, 512 * g : 512 * (g + 1)])
                wlds.append(wld)

        ident = const.tile([P, P], F32, name="ident")
        make_identity(nc, ident[:])
        ident_bf = const.tile([P, P], BF16, name="ident_bf")
        make_identity(nc, ident_bf[:])
        xi = const.tile([P, HALF], I32, name="xi")
        nc.gpsimd.iota(xi[:], pattern=[[2, 2], [4, HALF // 2]], base=1, channel_multiplier=0)
        ri = const.tile([P, 4], I32, name="ri")
        nc.gpsimd.iota(ri[:], pattern=[[1, 4]], base=0, channel_multiplier=0)
        x = const.tile([P, HALF], F32, name="x")
        nc.vector.tensor_copy(out=x[:], in_=xi[:])
        rho = const.tile([P, 3], F32, name="rho")
        for k in range(3):
            nc.vector.memset(rho[:, k : k + 1], float(A_CLASSES[k] - 2))
        neg_root2 = const.tile([P, 1], F32, name="neg_root2")
        nc.vector.tensor_scalar(
            out=neg_root2[:], in0=x[:, 0:1], scalar1=0.0, scalar2=-math.sqrt(2.0), op0=ALU.mult, op1=ALU.add
        )
        odq = const.tile([P, 4], F32, name="odq")
        nc.vector.tensor_scalar(out=odq[:], in0=ri[:], scalar1=2.0, scalar2=1.0, op0=ALU.mult, op1=ALU.add)
        odq128 = const.tile([P, 4], F32, name="odq128")
        nc.vector.tensor_scalar(out=odq128[:], in0=ri[:], scalar1=256.0, scalar2=128.0, op0=ALU.mult, op1=ALU.add)

        def small(dtype, name):
            return const.tile([P, PLANES], dtype, name=name)

        lam = lam_bf[:].rearrange("p r e -> p (r e)")

        def weave(first, second):
            for k in range(max(len(first), len(second))):
                for steps in (first, second):
                    if k < len(steps):
                        steps[k]()

        def frequency(k, label):
            mi = small(I32, "mi" + label)
            e1 = small(F32, "e1" + label)
            ml = small(F32, "ml" + label)
            mm = small(I32, "mm" + label)
            mh = small(F32, "mh" + label)
            steps = [
                lambda: nc.vector.tensor_scalar(out=mi[:], in0=lam, scalar1=k * C_ALL, scalar2=None, op0=ALU.mult),
                lambda: nc.vector.tensor_scalar(
                    out=mm[:],
                    in0=mi[:],
                    scalar1=TURN_SHIFT,
                    scalar2=TURN_SHIFT,
                    op0=ALU.logical_shift_left,
                    op1=ALU.arith_shift_right,
                ),
                lambda: nc.vector.scalar_tensor_tensor(
                    out=e1[:], in0=lam, scalar=k * C1, in1=mi[:], op0=ALU.mult, op1=ALU.subtract
                ),
                lambda: nc.vector.tensor_copy(out=mh[:], in_=mm[:]),
                lambda: nc.vector.scalar_tensor_tensor(
                    out=ml[:], in0=lam, scalar=k * C2, in1=e1[:], op0=ALU.mult, op1=ALU.add
                ),
            ]
            return mi, mh, ml, steps

        mi2, mh2, ml2, steps2 = frequency(2.0, "2")
        mi1, mh1, ml1, steps1 = frequency(1.0, "1")
        weave(steps2, steps1)
        ee = small(I32, "ee")
        nc.vector.tensor_scalar(
            out=ee[:], in0=mi2[:], scalar1=7, scalar2=TURN_MASK, op0=ALU.logical_shift_left, op1=ALU.bitwise_and
        )
        ef = small(F32, "ef")
        nc.vector.tensor_copy(out=ef[:], in_=ee[:])

        sc = const.tile([P, PLANES, 4, 3], F32, name="sc")
        bi = const.tile([P, PLANES, 4, 3], F32, name="bi")

        def phases(p0, p1, label):
            shape4 = [P, p1 - p0, 4, 3]
            pool = early["ph"]

            def tile4(dtype, name):
                return pool.tile(shape4, dtype, name=name + label)

            def flat(t):
                return t.rearrange("p a q r -> p (a q r)")

            def outer(o, v, tab):
                shape2 = list(o.shape)
                nc.vector.tensor_tensor(
                    out=o[:],
                    in0=v[:, p0:p1].unsqueeze(2).to_broadcast(shape2),
                    in1=tab[:].unsqueeze(1).to_broadcast(shape2),
                    op=ALU.mult,
                )

            def cross(o, a, b):
                nc.vector.tensor_tensor(
                    out=o[:],
                    in0=a[:].unsqueeze(3).to_broadcast(shape4),
                    in1=b[:].unsqueeze(2).to_broadcast(shape4),
                    op=ALU.add,
                )

            pq = pool.tile([P, p1 - p0, 4], F32, name="pq" + label)
            pr = pool.tile([P, p1 - p0, 3], F32, name="pr" + label)
            lq = pool.tile([P, p1 - p0, 4], F32, name="lq" + label)
            lr = pool.tile([P, p1 - p0, 3], F32, name="lr" + label)
            pa = tile4(F32, "pa")
            la = tile4(F32, "la")
            v1a = tile4(I32, "v1a")
            kua = tile4(I32, "kua")
            pba = tile4(I32, "pba")
            dd = tile4(F32, "dd")
            db = tile4(F32, "db")
            sc_p = flat(sc[:, p0:p1])
            return [
                lambda: outer(lq, ml2, odq128),
                lambda: outer(lr, ml1, rho),
                lambda: outer(pr, mh1, rho),
                lambda: outer(pq, ef, odq),
                lambda: cross(la, lq, lr),
                lambda: cross(pa, pq, pr),
                lambda: nc.vector.scalar_tensor_tensor(
                    out=flat(v1a[:]), in0=flat(pa[:]), scalar=5.0 * U, in1=flat(la[:]), op0=ALU.add, op1=ALU.add
                ),
                lambda: nc.vector.tensor_single_scalar(
                    out=flat(kua[:]), in_=flat(v1a[:]), scalar=0xFFFFFF - (U_INT - 1), op=ALU.bitwise_and
                ),
                lambda: nc.vector.tensor_single_scalar(
                    out=flat(pba[:]), in_=flat(v1a[:]), scalar=U_INT, op=ALU.bitwise_and
                ),
                lambda: nc.vector.tensor_tensor(
                    out=flat(dd[:]), in0=flat(pa[:]), in1=flat(kua[:]), op=ALU.subtract
                ),
                lambda: nc.vector.tensor_scalar(
                    out=sc_p, in0=flat(pba[:]), scalar1=-2.0 * PI_U / U, scalar2=PI_U, op0=ALU.mult, op1=ALU.add
                ),
                lambda: nc.vector.scalar_tensor_tensor(
                    out=flat(db[:]), in0=flat(dd[:]), scalar=4.0 * U, in1=flat(la[:]), op0=ALU.add, op1=ALU.add
                ),
                lambda: nc.vector.tensor_tensor(out=flat(bi[:, p0:p1]), in0=flat(db[:]), in1=sc_p, op=ALU.mult),
            ]

        t_tab = const.tile([P, PLANES, B], F32, name="t_tab")
        s_tab = const.tile([P, PASSES, B, 4], BF16, name="s_tab")

        v1s = {}

        def halves(tab):
            return tab.rearrange("p j (m h i) -> p j m h i", m=2, h=2)

        def products(c):
            v1 = early["tmp"].tile([P, 4, HALF], I32, name="v1")
            v1s[c] = v1

            def product(j):
                pl = 4 * c + j
                nc.vector.tensor_scalar(
                    out=v1[:, j, :], in0=x[:], scalar1=mh2[:, pl : pl + 1], scalar2=U / 2.0, op0=ALU.mult, op1=ALU.add
                )

            return [lambda j=j: product(j) for j in range(4)]

        def table(c):
            ff = early["tmp"].tile([P, 4, HALF], I32, name="ff")
            pb = early["tmp"].tile([P, 4, HALF], I32, name="pb")
            v1 = v1s[c]

            def upper(j):
                pl = 4 * c + j
                nc.vector.scalar_tensor_tensor(
                    out=halves(t_tab[:, pl : pl + 1, :])[:, 0, :, 1, :],
                    in0=x[:].rearrange("p (m i) -> p m i", m=2),
                    scalar=ml2[:, pl : pl + 1],
                    in1=ff[:, j, :].rearrange("p (m i) -> p m i", m=2),
                    op0=ALU.mult,
                    op1=ALU.add,
                )

            st = s_tab[:, c, :, :].rearrange("p (m h i) j -> p m h i j", m=2, h=2)
            pm = pb[:].rearrange("p j (m i) -> p m i j", m=2)

            def sign(h, source):
                nc.vector.tensor_scalar(
                    out=st[:, :, h, :, :], in0=source, scalar1=-2.0 / U, scalar2=1.0, op0=ALU.mult, op1=ALU.add
                )

            def lower():
                tv = halves(t_tab[:, 4 * c : 4 * c + 4, :])
                nc.vector.tensor_scalar(
                    out=tv[:, :, :, 0, :],
                    in0=tv[:, :, ::-1, 1, ::-1],
                    scalar1=-1.0,
                    scalar2=U,
                    op0=ALU.mult,
                    op1=ALU.add,
                )

            return (
                [
                    lambda: nc.vector.tensor_single_scalar(out=ff[:], in_=v1[:], scalar=U_INT - 1, op=ALU.bitwise_and),
                    lambda: nc.vector.tensor_single_scalar(out=pb[:], in_=v1[:], scalar=U_INT, op=ALU.bitwise_and),
                ]
                + (products(c + 1) if c + 1 < PASSES else [])
                + [lambda j=j: upper(j) for j in range(4)]
                + [lambda: sign(1, pm), lambda: sign(0, pm[:, ::-1, ::-1, :])]
                + ([lambda: quantise_w(c - 2)] if c >= 2 else [])
                + [lower]
            )

        w_codes = const.tile([P, PASSES, H], U32, name="w_codes", align_bytes=64)
        w_scales = const.tile([P, PASSES, H], U8, name="w_scales", align_bytes=64)
        wgs = {}

        def transpose_w(g):
            wv = wlds[g][:].rearrange("p m n -> p (m n)").bitcast(F32)
            wg = early["wstage"].tile([P, H, 2], F32, name="wg", align_bytes=64)
            wgs[g] = wg
            for mp in range(2):
                xt = psum.tile([P, 2, 2, P], F32, name="xt", tag="bank%d" % (4 + (2 * g + mp) % 4))
                for m2 in range(2):
                    for u in range(2):
                        c0 = 256 * (2 * mp + m2) + 128 * u
                        nc.tensor.transpose(xt[:, m2, u, :], wv[:, c0 : c0 + P], ident[:])
                nc.scalar.copy(
                    out=wg[:, 256 * mp : 256 * (mp + 1), :].rearrange("p (m h) u -> p m h u", m=2),
                    in_=xt[:].rearrange("p m u h -> p m h u"),
                )

        def quantise_w(g):
            nc.vector.quantize_mx(
                out=w_codes[:, g, :].bitcast(FP8X4),
                scales=w_scales[:, g, :],
                in_=wgs[g][:].rearrange("p h u -> p (h u)").bitcast(BF16),
            )

        e_first = const.tile([P, PLANES, 2, B], F32, name="e_first")
        z_keep = []
        for q in range(2):
            zk = const.tile([P, PLANES, 2, B], F32, name="z_keep%d" % q)
            z_keep.append(zk)

        units = [(q, c) for q in range(ROUNDS) for c in range(PASSES)]
        n_units = len(units)
        acc = {}
        zs = {}
        gs = {}
        zgs = {}

        def sine(dst, pl, q, r):
            k = A_CLASSES.index(r)
            nc.scalar.activation(
                out=dst,
                in_=t_tab[:, pl, :],
                func=ACT.Sin,
                bias=bi[:, pl, q, k : k + 1],
                scale=sc[:, pl, q, k : k + 1],
            )

        def halved(src, q):
            v = src.rearrange("p j s (m h i) -> p j s m h i", m=2, h=2)
            return v[:, :, :, :, q % 2, :].rearrange("p j s m i -> p j s i m")

        def even_place(q, planes):
            if q == 0:
                return e_first[:, planes, :, :]
            if q == 1:
                return late["e_keep"][:, planes, :, :]
            return z_keep[0][:, planes, :, :]

        def squares(q, c0, count):
            planes = slice(4 * c0, 4 * (c0 + count))
            ze = even_place(q, planes)

            def place(k):
                return ze[:, :, k, :].rearrange("p j (s i m) -> p j s i m", s=2, m=2)

            root2 = math.sqrt(2.0)
            if q == 1:
                src = halved(e_first[:, planes, :, :], q)
                dst = place(0)
                nc.scalar.activation(out=dst[:, :, 0:1], in_=src[:, :, 0:1], func=ACT.Square, scale=root2)
                nc.scalar.activation(
                    out=dst[:, :, 1:2], in_=src[:, :, 1:2], func=ACT.Square, scale=root2, bias=neg_root2[:]
                )
            elif q >= 2:
                src = halved(late["e_keep"][:, planes, :, :], q)
                nc.scalar.activation(out=place(0), in_=src, func=ACT.Square, scale=root2, bias=neg_root2[:])
            nc.scalar.activation(
                out=place(1), in_=halved(z_keep[q // 2][:, planes, :, :], q), func=ACT.Square, scale=root2
            )

        def sines(u):
            q, c = units[u]
            planes = slice(4 * c, 4 * c + 4)
            if q < 2:
                zo = z_keep[q][:, planes, :, :]
            else:
                zh = late["zpool"].tile([P, 4, 2, B], BF16, name="zh")
                zo = zh[:]
            ze = even_place(q, planes)
            zs[u] = (ze, zo)
            alone = u >= n_units - 2
            if q >= 2 and c % 2 == 0 and not alone:
                squares(q, c, 2)
            for j in range(4):
                for s in range(2):
                    sine(zo[:, j, s, :], 4 * c + j, q, 1 + 2 * s)
            if q == 0:
                for j in range(4):
                    sine(ze[:, j, 0, :], 4 * c + j, q, 0)
            if alone:
                squares(q, c, 1)
            elif q < 2 and c % 2 == 1:
                squares(q, c - 1, 2)

        def on_tensor(u):
            q, c = units[u]
            return 0 if q < 2 else 1 + c % 2

        def grouped_columns(u, first, count):
            return gs[u][:, first * B : (first + count) * B, :].rearrange("p (c i) t -> p c t i", i=4)

        def fours(z):
            return z.rearrange("p t s (c i) -> p (s c) t i", i=4)

        def regroup(u):
            grouped = gpool.tile([P, 512, 4], BF16, name="grouped", align_bytes=64)
            gs[u] = grouped
            ze, zo = zs[u]
            moved = on_tensor(u)
            if moved < 2:
                nc.vector.tensor_copy(out=grouped_columns(u, 2 + moved, 2 - moved), in_=fours(zo[:, :, moved:2, :]))
            if units[u][0] == 0:
                nc.vector.tensor_copy(out=grouped_columns(u, 0, 1), in_=fours(ze[:, :, 0:1, :]))
                nc.vector.tensor_scalar(
                    out=grouped_columns(u, 1, 1), in0=fours(ze[:, :, 1:2, :]), scalar1=-1.0, scalar2=None, op0=ALU.add
                )
            else:
                nc.vector.tensor_scalar(
                    out=grouped_columns(u, 0, 2), in0=fours(ze), scalar1=-1.0, scalar2=None, op0=ALU.add
                )

        def regroup_on_tensor(u):
            zg = psum.tile([P, on_tensor(u), 4 * B], BF16, name="zg", tag="bank%d" % (ACC_BANKS + u % 2))
            zgs[u] = zg
            zo = zs[u][1]
            for s in range(on_tensor(u)):
                nc.tensor.matmul(
                    zg[:, s, :].rearrange("p (b t) -> p t b", t=4),
                    lhsT=ident_bf[:],
                    rhs=zo[:, :, s, :],
                    start=True,
                    stop=True,
                )

        def signs(u):
            q, c = units[u]
            st = s_tab[:, c, :, :].rearrange("p b t -> p (b t)")
            two = st.unsqueeze(1).to_broadcast([P, 2, 4 * B])
            odd = gs[u][:, 2 * B : 4 * B, :].rearrange("p (r b) t -> p r (b t)", r=2)
            moved = on_tensor(u)
            if moved == 1:
                nc.vector.tensor_tensor(out=odd[:, 0, :], in0=zgs[u][:, 0, :], in1=st, op=ALU.mult)
                nc.vector.tensor_tensor(out=odd[:, 1, :], in0=odd[:, 1, :], in1=st, op=ALU.mult)
            else:
                nc.vector.tensor_tensor(out=odd, in0=odd if moved == 0 else zgs[u][:], in1=two, op=ALU.mult)
            if q == 0:
                g0 = gs[u][:, 0:B, :].rearrange("p b t -> p (b t)")
                nc.vector.tensor_tensor(out=g0, in0=g0, in1=st, op=ALU.mult)

        def quantise_and_multiply(u):
            q, c = units[u]
            s_codes = qpool.tile([P, 512], U32, name="s_codes", align_bytes=64)
            s_scales = qpool.tile([P, 512], U8, name="s_scales", align_bytes=64)
            nc.vector.quantize_mx(
                out=s_codes[:].bitcast(FP8X4),
                scales=s_scales[:],
                in_=gs[u][:].rearrange("p l t -> p (l t)"),
            )
            if c == 0:
                for m in range(4):
                    acc_m = psum.tile([P, 512], F32, name="acc", tag="bank%d" % ((4 * q + m) % ACC_BANKS))
                    acc[(q, m)] = acc_m
            for m in range(4):
                nc.tensor.matmul_mx(
                    out=acc[(q, m)][:],
                    lhsT=w_codes[:, c, m * P : (m + 1) * P].bitcast(FP8X4),
                    lhsT_scale=w_scales[:, c, m * P : (m + 1) * P],
                    rhs=s_codes[:].bitcast(FP8X4),
                    rhs_scale=s_scales[:],
                    start=(c == 0),
                    stop=(c == PASSES - 1),
                )

        def empty_bank(q, m, on_vector):
            o_sb = opool.tile([P, 512], F32, name="o_sb")
            dst = o_sb[:].rearrange("p (i s e o) -> p i s e o", s=2, e=2, o=2)
            src = acc[(q, m)][:].rearrange("p (o e s i) -> p i s e o", o=2, e=2, s=2)
            if on_vector:
                nc.vector.tensor_copy(out=dst, in_=src)
            else:
                nc.scalar.copy(out=dst, in_=src)
            nc.sync.dma_start(out=out[0, m * P : (m + 1) * P, 512 * q : 512 * (q + 1)], in_=o_sb[:])

        def iteration(u):
            q, c = units[u]
            if u + LEAD < n_units:
                sines(u + LEAD)
            regroup(u)
            if u + 1 < n_units and units[u + 1][0] >= 2:
                regroup_on_tensor(u + 1)
            if u >= 1:
                quantise_and_multiply(u - 1)
            signs(u)
            if q >= 1 and c == 0:
                for m in URGENT:
                    empty_bank(q - 1, m, True)
            if q >= 1 and c in (1, 2):
                empty_bank(q - 1, c + 1, False)

        with ExitStack() as first:
            early["tmp"] = first.enter_context(tc.tile_pool(name="tmp", bufs=2))
            early["ph"] = first.enter_context(tc.tile_pool(name="ph", bufs=1))
            early["wload"] = first.enter_context(tc.tile_pool(name="wload", bufs=W_AHEAD + 1))
            early["wstage"] = first.enter_context(tc.tile_pool(name="wstage", bufs=W_AHEAD + 2))
            load_w()
            for c in range(W_AHEAD):
                transpose_w(c)
            for step in products(0):
                step()
            weave(table(0), phases(0, 8, "0"))
            for c in range(PASSES):
                if c >= 1:
                    weave(table(c), phases(8, PLANES, "1") if c == 1 else [])
                if c < LEAD:
                    sines(c)
                if c + W_AHEAD < PASSES:
                    transpose_w(c + W_AHEAD)
            quantise_w(PASSES - 2)
            quantise_w(PASSES - 1)
        with tc.tile_pool(name="ekeep", bufs=1) as ekeep, tc.tile_pool(name="zpool", bufs=LEAD + 1) as zpool:
            late["zpool"] = zpool
            e_keep = ekeep.tile([P, PLANES, 2, B], F32, name="e_keep")
            late["e_keep"] = e_keep
            for u in range(n_units):
                iteration(u)
            quantise_and_multiply(n_units - 1)
            for m in range(4):
                empty_bank(ROUNDS - 1, m, m % 2 == 1)
